import numpy as np
import ml_dtypes


def mxq(x, axis, fmt="e4m3"):
    dtype, down = {"e4m3": (ml_dtypes.float8_e4m3fn, 7), "e5m2": (ml_dtypes.float8_e5m2, 14)}[fmt]
    v = np.moveaxis(np.asarray(x, np.float32).astype(ml_dtypes.bfloat16).astype(np.float64), axis, -1)
    blocks = v.reshape(v.shape[:-1] + (-1, 32))
    amax = np.abs(blocks).max(-1, keepdims=True)
    byte = np.maximum(np.where(amax > 0, np.frexp(amax)[1] - 1 + 127, 0) - down, 1)
    scale = np.exp2(byte - 127.0)
    codes = (blocks / scale).astype(np.float32).astype(dtype).astype(np.float64)
    return np.moveaxis((codes * scale).reshape(v.shape), -1, axis)


WIDE = False


def mx_kscale(k):
    if not WIDE:
        return np.ones(k)
    levels = np.array([10, -10, 5, -5, 0])
    a = np.random.permutation(np.resize(levels, k // 512 * 4)).reshape(k // 512, 4)
    idx = np.arange(k)
    return np.exp2(a[idx // 512, idx % 128 // 32])


BF16 = ml_dtypes.bfloat16


def bf(x):
    return np.asarray(x, np.float32).astype(BF16)


def f64(x):
    return np.asarray(x).astype(np.float64)


B, S, E, NH, DK, QB = 1, 1024, 1024, 16, 128, 512
HD = E // NH
SCALE = 1.0 / np.sqrt(HD)
LAYER_DEPTH = 0.25
QK_STD = 1.2 * (HD / E) ** 0.25


def setup_inputs():
    t = mx_kscale(E)
    return {"q": bf(np.random.standard_normal((B, S, E)) * QK_STD),
            "k": bf(np.random.standard_normal((B, S, E)) * QK_STD),
            "v": bf(np.random.standard_normal((B, S, E)) * t),
            "mem": bf(np.random.standard_normal((B, S, DK))),
            "attention_mask": bf(np.random.standard_normal((B, S)) * 0.3),
            "wo": bf(np.random.standard_normal((E, E)) * 2.0 / np.sqrt(E) / t[:, None]),
            "bo": bf(np.random.standard_normal(E) * 0.1)}


def reference(q, k, v, mem, attention_mask, wo, bo):
    qf, kf, mf, am = f64(q), f64(k), f64(mem), f64(attention_mask)
    kc = kf[:, :, :DK]
    vq = mxq(f64(v), 1, "e4m3")
    woq = mxq(f64(wo), 0, "e4m3")
    pos = np.arange(S)
    rows = []
    for r0 in range(0, S, QB):
        n = r0 + QB
        sc = qf[:, r0:n] @ kf[:, :n].transpose(0, 2, 1) * SCALE
        sc = sc + am[:, None, :n]
        sc = sc + np.where(pos[None, :n] > pos[r0:n, None], -np.inf, 0.0)
        sc = sc + mf[:, r0:n] @ kc[:, :n].transpose(0, 2, 1) * (SCALE * LAYER_DEPTH)
        e = np.exp(sc - sc.max(-1, keepdims=True))
        ctx = (mxq(e, 2, "e4m3") @ vq[:, :n]) / e.sum(-1, keepdims=True)
        rows.append((mxq(ctx, 2, "e4m3") @ woq) + f64(bo))
    return np.concatenate(rows, axis=1)

@@ -1,0 +1,399 @@
+import math
+from contextlib import ExitStack
+
+import concourse.mybir as mybir
+from concourse.masks import make_identity
+
+F32 = mybir.dt.float32
+BF16 = mybir.dt.bfloat16
+U32 = mybir.dt.uint32
+U8 = mybir.dt.uint8
+FP8X4 = mybir.dt.float8_e4m3fn_x4
+ALU = mybir.AluOpType
+ACT = mybir.ActivationFunctionType
+AXIS = mybir.AxisListType
+
+P = 128
+S = 1024
+E = 1024
+DK = 128
+TILES = S // P
+PACK = 4
+K_PASS = P * PACK
+BANK = 512
+SCALE = 1.0 / math.sqrt(64.0)
+LAYER_DEPTH = 0.25
+MASKED = -1.0e30
+WORD_BLOCKS = 3
+PLAIN_BLOCKS = 2
+
+QUERY_KEY_PAIRS = 512 * 512 + 512 * 1024
+FLOPS = 2 * QUERY_KEY_PAIRS * (E + DK + E) + 2 * S * E * E
+
+
+def tile_universalamrpalayer_pa_kernel(tc, q, k, v, mem, attention_mask, wo, bo, out):
+    nc = tc.nc
+
+    q_rows = q.flatten_outer_dims().rearrange("(t p) c -> t p c", p=P)
+    k_rows = k.flatten_outer_dims().rearrange("(t p) c -> t p c", p=P)
+    mem_rows = mem.flatten_outer_dims().rearrange("(t p) c -> p t c", p=P)
+    out_rows = out.flatten_outer_dims().rearrange("(t p) n -> t p n", p=P)
+    v_passes = v.flatten_outer_dims().rearrange("(g j p) c -> g p j c", j=PACK, p=P)
+    wo_passes = wo.rearrange("(g j p) n -> g p j n", j=PACK, p=P)
+
+    with ExitStack() as stack:
+        keep = stack.enter_context(tc.tile_pool(name="keep", bufs=1))
+        weights_in = stack.enter_context(tc.tile_pool(name="weights_in", bufs=8))
+        weights_grouped = stack.enter_context(tc.tile_pool(name="weights_grouped", bufs=3))
+        per_tile = stack.enter_context(tc.tile_pool(name="per_tile", bufs=3))
+        psum_transposes = stack.enter_context(tc.psum_pool(name="psum_transposes", bufs=3))
+        psum_scores = stack.enter_context(tc.psum_pool(name="psum_scores", bufs=2))
+        psum_mx = stack.enter_context(tc.psum_pool(name="psum_mx", bufs=3))
+
+        ident_f32 = keep.tile([P, P], F32)
+        make_identity(nc, ident_f32[:])
+        ident_bf16 = keep.tile([P, P], BF16)
+        make_identity(nc, ident_bf16[:])
+        ident_unscale = keep.tile([P, P], BF16)
+        nc.vector.tensor_scalar(
+            out=ident_unscale[:], in0=ident_bf16[:], scalar1=1.0 / SCALE, scalar2=None, op0=ALU.mult
+        )
+        causal = keep.tile([P, P], F32)
+        nc.gpsimd.memset(causal[:], 0.0)
+        nc.gpsimd.affine_select(
+            out=causal[:],
+            in_=causal[:],
+            compare_op=ALU.is_ge,
+            fill=MASKED,
+            base=0,
+            pattern=[[-1, P]],
+            channel_multiplier=1,
+        )
+        warm = keep.tile([P, 1], F32)
+        nc.vector.memset(warm[:], 0.0)
+        nc.scalar.activation(out=warm[:], in_=warm[:], func=ACT.Exp)
+
+        q_raw = keep.tile([P, TILES, E], BF16)
+        k_raw = keep.tile([P, TILES, E], BF16)
+        mem_raw = keep.tile([P, TILES, DK], BF16)
+        q_t = keep.tile([P, TILES, BANK], F32)
+        k_t_words = keep.tile([P, WORD_BLOCKS, S], F32)
+        k_t_plain = keep.tile([P, PLAIN_BLOCKS, S], BF16)
+        mem_t = keep.tile([P, S], BF16)
+        mask_rows = keep.tile([P, S], BF16)
+        mask_diag = keep.tile([P, TILES, P], BF16)
+        bias_rows = keep.tile([P, E], BF16)
+        v_codes = keep.tile([P, S // K_PASS, E], U32, align_bytes=64)
+        v_scales = keep.tile([P, S // K_PASS, E], U8, align_bytes=64)
+        wo_codes = keep.tile([P, E // K_PASS, E], U32, align_bytes=64)
+        wo_scales = keep.tile([P, E // K_PASS, E], U8, align_bytes=64)
+        e_slots = sum(passes_of(t) for t in range(TILES))
+        e_grouped = keep.tile([P, e_slots, P, PACK], BF16, align_bytes=64)
+        nc.vector.memset(e_grouped[:], 0.0)
+        e_codes = keep.tile([P, e_slots, P], U32, align_bytes=64)
+        e_scales = keep.tile([P, e_slots, P], U8, align_bytes=64)
+
+        last = TILES - 1
+        nc.sync.dma_start(out=q_raw[:, last, :], in_=q_rows[last])
+        for t in range(TILES // 2):
+            nc.sync.dma_start(out=k_raw[:, t, :], in_=k_rows[t])
+        nc.sync.dma_start(out=mem_raw[:], in_=mem_rows)
+        for t in range(TILES // 2, TILES):
+            nc.sync.dma_start(out=k_raw[:, t, :], in_=k_rows[t])
+        v_pieces = load_weight(nc, weights_in, v_passes)
+        nc.sync.dma_start(out=q_raw[:, last - 1, :], in_=q_rows[last - 1])
+        wo_pieces = load_weight(nc, weights_in, wo_passes)
+        for t in range(last - 2, -1, -1):
+            nc.sync.dma_start(out=q_raw[:, t, :], in_=q_rows[t])
+        nc.scalar.dma_start(
+            out=mask_rows[:], in_=attention_mask.rearrange("b s -> (b s)").partition_broadcast(P)
+        )
+        nc.scalar.dma_start(out=bias_rows[:], in_=bo.partition_broadcast(P))
+
+        nc.vector.tensor_tensor(
+            out=mask_diag[:],
+            in0=mask_rows[:].rearrange("p (t r) -> p t r", r=P),
+            in1=causal[:].unsqueeze(1).to_broadcast([P, TILES, P]),
+            op=ALU.add,
+        )
+
+        def transpose_rows(rows):
+            bank = psum_transposes.tile([P, BANK], F32, tag="transposes")
+            words = rows.bitcast(F32)
+            for w in range(WORD_BLOCKS):
+                nc.tensor.transpose(
+                    out=bank[:, w * P : (w + 1) * P],
+                    in_=words[:, (w + 1) * P : (w + 2) * P],
+                    identity=ident_f32[:],
+                )
+            plain = bank[:, WORD_BLOCKS * P :].bitcast(BF16)
+            for h in range(PLAIN_BLOCKS):
+                nc.tensor.transpose(
+                    out=plain[:, h * P : (h + 1) * P],
+                    in_=rows[:, h * P : (h + 1) * P],
+                    identity=ident_bf16[:],
+                )
+            return bank
+
+        def transpose_queries(t):
+            bank = transpose_rows(q_raw[:, t, :])
+            nc.scalar.copy(out=q_t[:, t, :], in_=bank[:])
+
+        def transpose_keys(t):
+            bank = transpose_rows(k_raw[:, t, :])
+            keys = slice(t * P, (t + 1) * P)
+            word_keys = slice(t * P // 2, (t + 1) * P // 2)
+            moves = (
+                (k_t_words[:, :, keys], bank[:, : WORD_BLOCKS * P].rearrange("p (w r) -> p w r", w=WORD_BLOCKS)),
+                (
+                    k_t_plain[:].bitcast(F32)[:, :, word_keys],
+                    bank[:, WORD_BLOCKS * P :].rearrange("p (h r) -> p h r", h=PLAIN_BLOCKS),
+                ),
+            )
+            for dst, src in moves:
+                if t % 2 == 0:
+                    nc.scalar.copy(out=dst, in_=src)
+                else:
+                    nc.vector.tensor_copy(out=dst, in_=src)
+
+        def transpose_mem():
+            bank = psum_transposes.tile([P, TILES, P], BF16, tag="transposes")
+            for t in range(TILES):
+                nc.tensor.transpose(out=bank[:, t, :], in_=mem_raw[:, t, :], identity=ident_bf16[:])
+            nc.vector.tensor_scalar(
+                out=mem_t[:],
+                in0=bank[:].rearrange("p t r -> p (t r)"),
+                scalar1=LAYER_DEPTH,
+                scalar2=None,
+                op0=ALU.mult,
+            )
+
+        def quantise_weight(pieces, codes, scales, copy):
+            previous = None
+            for g, cols, raw in pieces:
+                grouped = weights_grouped.tile([P, BANK, PACK], BF16, align_bytes=64)
+                copy(
+                    out=grouped[:].rearrange("p (c i) j -> p c j i", i=4),
+                    in_=raw[:].rearrange("p j (c i) -> p c j i", i=4),
+                )
+                if previous is not None:
+                    quantise_piece(nc, previous, codes, scales)
+                previous = (g, cols, grouped)
+            quantise_piece(nc, previous, codes, scales)
+
+        e_of = {}
+        rinv_of = {}
+
+        def scores_and_softmax(t):
+            n_keys = (t + 1) * P
+            n_banks = (n_keys + BANK - 1) // BANK
+            queries = slice(t * P, (t + 1) * P)
+            q_words = q_t[:, t, : WORD_BLOCKS * P].bitcast(BF16).rearrange(
+                "p (w r e) -> p w r e", w=WORD_BLOCKS, e=2
+            )
+            q_plain = q_t[:, t, WORD_BLOCKS * P :].bitcast(BF16)
+            k_words = k_t_words[:].bitcast(BF16).rearrange("p w (r e) -> p w r e", e=2)
+
+            row_max = per_tile.tile([P, 2], F32)
+            neg_max = per_tile.tile([P, 1], F32)
+            row_sum = per_tile.tile([P, 2], F32)
+            total = per_tile.tile([P, 1], F32)
+            rinv = per_tile.tile([P, 1], F32)
+            e_sb = per_tile.tile([P, S], BF16)
+
+            banks = []
+            for b in range(n_banks):
+                lo = b * BANK
+                n = min(BANK, n_keys - lo)
+                keys = slice(lo, lo + n)
+                acc = psum_scores.tile([P, BANK], F32, tag="scores")
+                nc.tensor.matmul(
+                    out=acc[:, :n], lhsT=q_plain[:, 0:P], rhs=k_t_plain[:, 0, keys], start=True, stop=False
+                )
+                below = n - P if b == n_banks - 1 else n
+                if below > 0:
+                    nc.tensor.matmul(
+                        out=acc[:, :below],
+                        lhsT=ident_unscale[:],
+                        rhs=mask_rows[:, lo : lo + below],
+                        start=False,
+                        stop=False,
+                    )
+                if b == n_banks - 1:
+                    nc.tensor.matmul(
+                        out=acc[:, below:n], lhsT=ident_unscale[:], rhs=mask_diag[:, t, :], start=False, stop=False
+                    )
+                nc.tensor.matmul(
+                    out=acc[:, :n], lhsT=q_plain[:, P : 2 * P], rhs=k_t_plain[:, 1, keys], start=False, stop=False
+                )
+                for w in range(WORD_BLOCKS):
+                    for half in range(2):
+                        nc.tensor.matmul(
+                            out=acc[:, :n],
+                            lhsT=q_words[:, w, :, half],
+                            rhs=k_words[:, w, keys, half],
+                            start=False,
+                            stop=False,
+                        )
+                nc.tensor.matmul(
+                    out=acc[:, :n], lhsT=mem_t[:, queries], rhs=k_t_plain[:, 0, keys], start=False, stop=True
+                )
+                nc.vector.tensor_reduce(out=row_max[:, b : b + 1], in_=acc[:, :n], axis=AXIS.X, op=ALU.max)
+                banks.append((acc, keys, n))
+
+            if n_banks == 2:
+                nc.vector.tensor_scalar(
+                    out=neg_max[:],
+                    in0=row_max[:, 0:1],
+                    scalar1=row_max[:, 1:2],
+                    scalar2=-SCALE,
+                    op0=ALU.max,
+                    op1=ALU.mult,
+                )
+            else:
+                nc.vector.tensor_scalar(
+                    out=neg_max[:], in0=row_max[:, 0:1], scalar1=-SCALE, scalar2=None, op0=ALU.mult
+                )
+            for b, (acc, keys, n) in enumerate(banks):
+                nc.scalar.activation(
+                    out=e_sb[:, keys],
+                    in_=acc[:, :n],
+                    func=ACT.Exp,
+                    bias=neg_max[:, 0:1],
+                    scale=SCALE,
+                    accum_out=row_sum[:, b : b + 1],
+                )
+            nc.vector.tensor_reduce(out=total[:], in_=row_sum[:, :n_banks], axis=AXIS.X, op=ALU.add)
+            nc.vector.reciprocal(out=rinv[:], in_=total[:])
+            e_of[t] = e_sb
+            rinv_of[t] = rinv
+
+        rinv_rows_of = {}
+
+        def transpose_e(t):
+            e_sb = e_of[t]
+            bank = psum_transposes.tile([P, TILES, P], BF16, tag="transposes")
+            for kt in range(t + 1):
+                nc.tensor.transpose(out=bank[:, kt, :], in_=e_sb[:, kt * P : (kt + 1) * P], identity=ident_bf16[:])
+            spread = psum_transposes.tile([P, P], F32, tag="transposes")
+            nc.tensor.transpose(out=spread[:], in_=rinv_of[t][:, 0:1].to_broadcast([P, P]), identity=ident_f32[:])
+
+            first = first_slot(t)
+            for g in range(passes_of(t)):
+                key_tiles = min(PACK, t + 1 - g * PACK)
+                nc.scalar.copy(
+                    out=e_grouped[:, first + g, :, :key_tiles],
+                    in_=bank[:, g * PACK : g * PACK + key_tiles, :].rearrange("p j r -> p r j"),
+                )
+            rinv_rows = per_tile.tile([P, P], F32)
+            nc.scalar.copy(out=rinv_rows[:], in_=spread[:])
+            rinv_rows_of[t] = rinv_rows
+            slots = slice(first, first + passes_of(t))
+            nc.vector.quantize_mx(
+                out=e_codes[:, slots, :].rearrange("p s r -> p (s r)").bitcast(FP8X4),
+                scales=e_scales[:, slots, :].rearrange("p s r -> p (s r)"),
+                in_=e_grouped[:, slots, :, :].rearrange("p s r j -> p (s r j)"),
+            )
+
+        ctx_of = {}
+
+        def context(t):
+            rinv_rows = rinv_rows_of[t]
+            ctx_grouped = per_tile.tile([P, E // K_PASS, P, PACK], BF16, align_bytes=64)
+            ctx_codes = per_tile.tile([P, E // K_PASS, P], U32, align_bytes=64)
+            ctx_scales = per_tile.tile([P, E // K_PASS, P], U8, align_bytes=64)
+            first = first_slot(t)
+            n_passes = passes_of(t)
+            for g_out in range(E // K_PASS):
+                acc = psum_mx.tile([P, PACK, P], F32, tag="mx")
+                for j in range(PACK):
+                    channels = slice((g_out * PACK + j) * P, (g_out * PACK + j + 1) * P)
+                    for g in range(n_passes):
+                        nc.tensor.matmul_mx(
+                            out=acc[:, j, :],
+                            lhsT=v_codes[:, g, channels].bitcast(FP8X4),
+                            lhsT_scale=v_scales[:, g, channels],
+                            rhs=e_codes[:, first + g, :].bitcast(FP8X4),
+                            rhs_scale=e_scales[:, first + g, :],
+                            start=(g == 0),
+                            stop=(g == n_passes - 1),
+                        )
+                nc.vector.tensor_tensor(
+                    out=ctx_grouped[:, g_out, :, :],
+                    in0=acc[:].rearrange("p j r -> p r j"),
+                    in1=rinv_rows[:].unsqueeze(2).to_broadcast([P, P, PACK]),
+                    op=ALU.mult,
+                )
+            nc.vector.quantize_mx(
+                out=ctx_codes[:].rearrange("p g r -> p (g r)").bitcast(FP8X4),
+                scales=ctx_scales[:].rearrange("p g r -> p (g r)"),
+                in_=ctx_grouped[:].rearrange("p g r j -> p (g r j)"),
+            )
+            ctx_of[t] = (ctx_codes, ctx_scales)
+
+        def project(t):
+            ctx_codes, ctx_scales = ctx_of[t]
+            out_sb = per_tile.tile([P, E], F32)
+            for h in range(E // BANK):
+                cols = slice(h * BANK, (h + 1) * BANK)
+                acc = psum_mx.tile([P, BANK], F32, tag="mx")
+                for g in range(E // K_PASS):
+                    nc.tensor.matmul_mx(
+                        out=acc[:],
+                        lhsT=ctx_codes[:, g, :].bitcast(FP8X4),
+                        lhsT_scale=ctx_scales[:, g, :],
+                        rhs=wo_codes[:, g, cols].bitcast(FP8X4),
+                        rhs_scale=wo_scales[:, g, cols],
+                        start=(g == 0),
+                        stop=(g == E // K_PASS - 1),
+                    )
+                nc.vector.tensor_tensor(out=out_sb[:, cols], in0=acc[:], in1=bias_rows[:, cols], op=ALU.add)
+            nc.sync.dma_start(out=out_rows[t], in_=out_sb[:])
+
+        order = list(range(TILES - 1, -1, -1))
+        transpose_queries(order[0])
+        for t in range(TILES):
+            transpose_keys(t)
+        transpose_mem()
+        quantise_weight(v_pieces, v_codes, v_scales, nc.vector.tensor_copy)
+        for step in range(TILES + 2):
+            if step + 1 < TILES:
+                transpose_queries(order[step + 1])
+            if 1 <= step <= TILES:
+                transpose_e(order[step - 1])
+            if step < TILES:
+                scores_and_softmax(order[step])
+            if step == 1:
+                quantise_weight(wo_pieces, wo_codes, wo_scales, nc.scalar.copy)
+            if step >= 2:
+                project(order[step - 2])
+            if 1 <= step <= TILES:
+                context(order[step - 1])
+
+
+def passes_of(t):
+    return (t * P) // K_PASS + 1
+
+
+def first_slot(t):
+    return sum(passes_of(u) for u in range(t))
+
+
+def load_weight(nc, pool, passes):
+    pieces = []
+    for g in range(passes.shape[0]):
+        for h in range(passes.shape[3] // BANK):
+            cols = slice(h * BANK, (h + 1) * BANK)
+            raw = pool.tile([P, PACK, BANK], BF16, tag="weight_piece")
+            nc.sync.dma_start(out=raw[:], in_=passes[g][:, :, cols])
+            pieces.append((g, cols, raw))
+    return pieces
+
+
+def quantise_piece(nc, piece, codes, scales):
+    g, cols, grouped = piece
+    nc.vector.quantize_mx(
+        out=codes[:, g, cols].bitcast(FP8X4),
+        scales=scales[:, g, cols],
+        in_=grouped[:].rearrange("p c j -> p (c j)"),
+    )

@@ -8,6 +8,7 @@ F32 = mybir.dt.float32
 BF16 = mybir.dt.bfloat16
 U32 = mybir.dt.uint32
 U8 = mybir.dt.uint8
+I32 = mybir.dt.int32
 FP8X4 = mybir.dt.float8_e4m3fn_x4
 ALU = mybir.AluOpType
 ACT = mybir.ActivationFunctionType
@@ -21,14 +22,29 @@ TILES = S // P
 PACK = 4
 K_PASS = P * PACK
 BANK = 512
+BANK_TILES = BANK // P
 SCALE = 1.0 / math.sqrt(64.0)
 LAYER_DEPTH = 0.25
 MASKED = -1.0e30
 WORD_BLOCKS = 3
 PLAIN_BLOCKS = 2
+CONTEXT_LAG = 1
+PROJECT_LAG = 3
 
 QUERY_KEY_PAIRS = 512 * 512 + 512 * 1024
 FLOPS = 2 * QUERY_KEY_PAIRS * (E + DK + E) + 2 * S * E * E
+
+
+def passes_of(t):
+    return (t * P) // K_PASS + 1
+
+
+def first_slot(t):
+    return sum(passes_of(u) for u in range(t))
+
+
+def banks_of(t):
+    return t // BANK_TILES + 1
 
 
 def tile_universalamrpalayer_pa_kernel(tc, q, k, v, mem, attention_mask, wo, bo, out):
@@ -45,33 +61,11 @@ def tile_universalamrpalayer_pa_kernel(tc, q, k, v, mem, attention_mask, wo, bo,
         keep = stack.enter_context(tc.tile_pool(name="keep", bufs=1))
         weights_in = stack.enter_context(tc.tile_pool(name="weights_in", bufs=8))
         weights_grouped = stack.enter_context(tc.tile_pool(name="weights_grouped", bufs=3))
-        per_tile = stack.enter_context(tc.tile_pool(name="per_tile", bufs=3))
-        psum_transposes = stack.enter_context(tc.psum_pool(name="psum_transposes", bufs=3))
-        psum_scores = stack.enter_context(tc.psum_pool(name="psum_scores", bufs=2))
-        psum_mx = stack.enter_context(tc.psum_pool(name="psum_mx", bufs=3))
-
-        ident_f32 = keep.tile([P, P], F32)
-        make_identity(nc, ident_f32[:])
-        ident_bf16 = keep.tile([P, P], BF16)
-        make_identity(nc, ident_bf16[:])
-        ident_unscale = keep.tile([P, P], BF16)
-        nc.vector.tensor_scalar(
-            out=ident_unscale[:], in0=ident_bf16[:], scalar1=1.0 / SCALE, scalar2=None, op0=ALU.mult
-        )
-        causal = keep.tile([P, P], F32)
-        nc.gpsimd.memset(causal[:], 0.0)
-        nc.gpsimd.affine_select(
-            out=causal[:],
-            in_=causal[:],
-            compare_op=ALU.is_ge,
-            fill=MASKED,
-            base=0,
-            pattern=[[-1, P]],
-            channel_multiplier=1,
-        )
-        warm = keep.tile([P, 1], F32)
-        nc.vector.memset(warm[:], 0.0)
-        nc.scalar.activation(out=warm[:], in_=warm[:], func=ACT.Exp)
+        per_tile = stack.enter_context(tc.tile_pool(name="per_tile", bufs=PROJECT_LAG + 1))
+        psum_transposes = stack.enter_context(tc.psum_pool(name="psum_transposes", bufs=2))
+        psum_scores = stack.enter_context(tc.psum_pool(name="psum_scores", bufs=3))
+        psum_shared = stack.enter_context(tc.psum_pool(name="psum_shared", bufs=3))
+        stack.enter_context(tc.manual_schedule())
 
         q_raw = keep.tile([P, TILES, E], BF16)
         k_raw = keep.tile([P, TILES, E], BF16)
@@ -80,45 +74,84 @@ def tile_universalamrpalayer_pa_kernel(tc, q, k, v, mem, attention_mask, wo, bo,
         k_t_words = keep.tile([P, WORD_BLOCKS, S], F32)
         k_t_plain = keep.tile([P, PLAIN_BLOCKS, S], BF16)
         mem_t = keep.tile([P, S], BF16)
-        mask_rows = keep.tile([P, S], BF16)
-        mask_diag = keep.tile([P, TILES, P], BF16)
-        bias_rows = keep.tile([P, E], BF16)
+        mask_row = keep.tile([P, S], BF16)
+        bias_row = keep.tile([P, E], BF16)
+        bias_rows = keep.tile([P, E], F32)
         v_codes = keep.tile([P, S // K_PASS, E], U32, align_bytes=64)
         v_scales = keep.tile([P, S // K_PASS, E], U8, align_bytes=64)
         wo_codes = keep.tile([P, E // K_PASS, E], U32, align_bytes=64)
         wo_scales = keep.tile([P, E // K_PASS, E], U8, align_bytes=64)
-        e_slots = sum(passes_of(t) for t in range(TILES))
+        e_slots = first_slot(TILES)
         e_grouped = keep.tile([P, e_slots, P, PACK], BF16, align_bytes=64)
-        nc.vector.memset(e_grouped[:], 0.0)
         e_codes = keep.tile([P, e_slots, P], U32, align_bytes=64)
         e_scales = keep.tile([P, e_slots, P], U8, align_bytes=64)
 
-        last = TILES - 1
-        nc.sync.dma_start(out=q_raw[:, last, :], in_=q_rows[last])
-        for t in range(TILES // 2):
+        nc.gpsimd.memset(bias_row[:].bitcast(F32), 0.0)
+        nc.vector.memset(mask_row[:].bitcast(I32), 0)
+
+        def load_weight(passes):
+            pieces = []
+            for g in range(passes.shape[0]):
+                pieces.append([])
+                for h in range(passes.shape[3] // BANK):
+                    cols = slice(h * BANK, (h + 1) * BANK)
+                    raw = weights_in.tile([P, PACK, BANK], BF16, tag="weight_piece")
+                    nc.sync.dma_start(out=raw[:], in_=passes[g][:, :, cols])
+                    pieces[g].append((cols, raw))
+            return pieces
+
+        order = list(range(TILES - 1, -1, -1))
+        nc.sync.dma_start(out=bias_row[0:1, :], in_=bo.unsqueeze(0))
+        nc.sync.dma_start(out=q_raw[:, order[0], :], in_=q_rows[order[0]])
+        nc.sync.dma_start(out=mask_row[0:1, :], in_=attention_mask)
+        for t in range(BANK_TILES):
             nc.sync.dma_start(out=k_raw[:, t, :], in_=k_rows[t])
         nc.sync.dma_start(out=mem_raw[:], in_=mem_rows)
-        for t in range(TILES // 2, TILES):
+        for t in range(BANK_TILES, TILES):
             nc.sync.dma_start(out=k_raw[:, t, :], in_=k_rows[t])
-        v_pieces = load_weight(nc, weights_in, v_passes)
-        nc.sync.dma_start(out=q_raw[:, last - 1, :], in_=q_rows[last - 1])
-        wo_pieces = load_weight(nc, weights_in, wo_passes)
-        for t in range(last - 2, -1, -1):
+        nc.sync.dma_start(out=q_raw[:, order[1], :], in_=q_rows[order[1]])
+        v_pieces = load_weight(v_passes)
+        nc.sync.dma_start(out=q_raw[:, order[2], :], in_=q_rows[order[2]])
+        wo_pieces = load_weight(wo_passes)
+        for t in order[3:]:
             nc.sync.dma_start(out=q_raw[:, t, :], in_=q_rows[t])
-        nc.scalar.dma_start(
-            out=mask_rows[:], in_=attention_mask.rearrange("b s -> (b s)").partition_broadcast(P)
-        )
-        nc.scalar.dma_start(out=bias_rows[:], in_=bo.partition_broadcast(P))
 
-        nc.vector.tensor_tensor(
-            out=mask_diag[:],
-            in0=mask_rows[:].rearrange("p (t r) -> p t r", r=P),
-            in1=causal[:].unsqueeze(1).to_broadcast([P, TILES, P]),
-            op=ALU.add,
+        ident_f32 = keep.tile([P, P], F32)
+        make_identity(nc, ident_f32[:])
+        ident_bf16 = keep.tile([P, P], BF16)
+        make_identity(nc, ident_bf16[:])
+        causal_f32 = keep.tile([P, P], F32)
+        nc.gpsimd.memset(causal_f32[:], 0.0)
+        nc.gpsimd.affine_select(
+            out=causal_f32[:],
+            in_=causal_f32[:],
+            compare_op=ALU.is_ge,
+            fill=MASKED,
+            base=0,
+            pattern=[[-1, P]],
+            channel_multiplier=1,
         )
+        causal = keep.tile([P, P], BF16)
+        nc.gpsimd.tensor_copy(out=causal[:], in_=causal_f32[:])
+        ones = keep.tile([P, P], BF16)
+        nc.vector.memset(ones[:], 1.0)
+        unscale = keep.tile([P, P], BF16)
+        nc.vector.memset(unscale[:], 1.0 / SCALE)
+        nc.vector.memset(e_grouped[:].bitcast(I32), 0)
+        minus_one = keep.tile([P, 1], F32)
+        nc.gpsimd.memset(minus_one[:], -1.0)
+        warm = keep.tile([P, 1], F32)
+        nc.vector.memset(warm[:], 0.0)
+        nc.scalar.activation(out=warm[:], in_=warm[:], func=ACT.Exp)
 
-        def transpose_rows(rows):
-            bank = psum_transposes.tile([P, BANK], F32, tag="transposes")
+        def spread_bias():
+            for h in range(E // BANK):
+                cols = slice(h * BANK, (h + 1) * BANK)
+                bank = psum_shared.tile([P, BANK], F32, tag="shared")
+                nc.tensor.matmul(out=bank[:], lhsT=ones[:], rhs=bias_row[:, cols], start=True, stop=True)
+                nc.vector.tensor_copy(out=bias_rows[:, cols], in_=bank[:])
+
+        def transpose_rows(rows, bank):
             words = rows.bitcast(F32)
             for w in range(WORD_BLOCKS):
                 nc.tensor.transpose(
@@ -133,14 +166,15 @@ def tile_universalamrpalayer_pa_kernel(tc, q, k, v, mem, attention_mask, wo, bo,
                     in_=rows[:, h * P : (h + 1) * P],
                     identity=ident_bf16[:],
                 )
-            return bank
 
         def transpose_queries(t):
-            bank = transpose_rows(q_raw[:, t, :])
+            bank = psum_transposes.tile([P, BANK], F32, tag="transposes")
+            transpose_rows(q_raw[:, t, :], bank)
             nc.scalar.copy(out=q_t[:, t, :], in_=bank[:])
 
         def transpose_keys(t):
-            bank = transpose_rows(k_raw[:, t, :])
+            bank = psum_shared.tile([P, BANK], F32, tag="shared")
+            transpose_rows(k_raw[:, t, :], bank)
             keys = slice(t * P, (t + 1) * P)
             word_keys = slice(t * P // 2, (t + 1) * P // 2)
             moves = (
@@ -168,25 +202,45 @@ def tile_universalamrpalayer_pa_kernel(tc, q, k, v, mem, attention_mask, wo, bo,
                 op0=ALU.mult,
             )
 
-        def quantise_weight(pieces, codes, scales, copy):
-            previous = None
-            for g, cols, raw in pieces:
+        def quantise_weight(pieces, codes, scales):
+            regrouped = []
+            for cols, raw in pieces:
                 grouped = weights_grouped.tile([P, BANK, PACK], BF16, align_bytes=64)
-                copy(
+                nc.vector.tensor_copy(
                     out=grouped[:].rearrange("p (c i) j -> p c j i", i=4),
                     in_=raw[:].rearrange("p j (c i) -> p c j i", i=4),
                 )
-                if previous is not None:
-                    quantise_piece(nc, previous, codes, scales)
-                previous = (g, cols, grouped)
-            quantise_piece(nc, previous, codes, scales)
+                regrouped.append((cols, grouped))
+            for cols, grouped in regrouped:
+                nc.vector.quantize_mx(
+                    out=codes[:, cols].bitcast(FP8X4),
+                    scales=scales[:, cols],
+                    in_=grouped[:].rearrange("p c j -> p (c j)"),
+                )
 
-        e_of = {}
-        rinv_of = {}
+        softmax_of = {}
 
-        def scores_and_softmax(t):
-            n_keys = (t + 1) * P
-            n_banks = (n_keys + BANK - 1) // BANK
+        def start_softmax(t):
+            row_max = per_tile.tile([P, 2], F32)
+            neg_max = per_tile.tile([P, 1], F32)
+            row_sum = per_tile.tile([P, 2], F32)
+            total = per_tile.tile([P, 1], F32)
+            rinv = per_tile.tile([P, 1], F32)
+            e_sb = per_tile.tile([P, S], BF16)
+            softmax_of[t] = {
+                "row_max": row_max,
+                "neg_max": neg_max,
+                "row_sum": row_sum,
+                "total": total,
+                "rinv": rinv,
+                "e": e_sb,
+                "banks": [],
+            }
+
+        def score_bank(t, b):
+            lo = b * BANK
+            n = min(BANK, (t + 1) * P - lo)
+            keys = slice(lo, lo + n)
             queries = slice(t * P, (t + 1) * P)
             q_words = q_t[:, t, : WORD_BLOCKS * P].bitcast(BF16).rearrange(
                 "p (w r e) -> p w r e", w=WORD_BLOCKS, e=2
@@ -194,89 +248,81 @@ def tile_universalamrpalayer_pa_kernel(tc, q, k, v, mem, attention_mask, wo, bo,
             q_plain = q_t[:, t, WORD_BLOCKS * P :].bitcast(BF16)
             k_words = k_t_words[:].bitcast(BF16).rearrange("p w (r e) -> p w r e", e=2)
 
-            row_max = per_tile.tile([P, 2], F32)
-            neg_max = per_tile.tile([P, 1], F32)
-            row_sum = per_tile.tile([P, 2], F32)
-            total = per_tile.tile([P, 1], F32)
-            rinv = per_tile.tile([P, 1], F32)
-            e_sb = per_tile.tile([P, S], BF16)
-
-            banks = []
-            for b in range(n_banks):
-                lo = b * BANK
-                n = min(BANK, n_keys - lo)
-                keys = slice(lo, lo + n)
-                acc = psum_scores.tile([P, BANK], F32, tag="scores")
+            acc = psum_scores.tile([P, BANK], F32, tag="scores")
+            for h in range(PLAIN_BLOCKS):
                 nc.tensor.matmul(
-                    out=acc[:, :n], lhsT=q_plain[:, 0:P], rhs=k_t_plain[:, 0, keys], start=True, stop=False
+                    out=acc[:, :n],
+                    lhsT=q_plain[:, h * P : (h + 1) * P],
+                    rhs=k_t_plain[:, h, keys],
+                    start=(h == 0),
+                    stop=False,
                 )
-                below = n - P if b == n_banks - 1 else n
-                if below > 0:
+            for w in range(WORD_BLOCKS):
+                for half in range(2):
                     nc.tensor.matmul(
-                        out=acc[:, :below],
-                        lhsT=ident_unscale[:],
-                        rhs=mask_rows[:, lo : lo + below],
+                        out=acc[:, :n],
+                        lhsT=q_words[:, w, :, half],
+                        rhs=k_words[:, w, keys, half],
                         start=False,
                         stop=False,
                     )
-                if b == n_banks - 1:
-                    nc.tensor.matmul(
-                        out=acc[:, below:n], lhsT=ident_unscale[:], rhs=mask_diag[:, t, :], start=False, stop=False
-                    )
-                nc.tensor.matmul(
-                    out=acc[:, :n], lhsT=q_plain[:, P : 2 * P], rhs=k_t_plain[:, 1, keys], start=False, stop=False
-                )
-                for w in range(WORD_BLOCKS):
-                    for half in range(2):
-                        nc.tensor.matmul(
-                            out=acc[:, :n],
-                            lhsT=q_words[:, w, :, half],
-                            rhs=k_words[:, w, keys, half],
-                            start=False,
-                            stop=False,
-                        )
-                nc.tensor.matmul(
-                    out=acc[:, :n], lhsT=mem_t[:, queries], rhs=k_t_plain[:, 0, keys], start=False, stop=True
-                )
-                nc.vector.tensor_reduce(out=row_max[:, b : b + 1], in_=acc[:, :n], axis=AXIS.X, op=ALU.max)
-                banks.append((acc, keys, n))
+            nc.tensor.matmul(out=acc[:, :n], lhsT=unscale[:], rhs=mask_row[:, keys], start=False, stop=False)
+            if b == banks_of(t) - 1:
+                nc.tensor.matmul(out=acc[:, n - P : n], lhsT=ident_bf16[:], rhs=causal[:], start=False, stop=False)
+            nc.tensor.matmul(
+                out=acc[:, :n], lhsT=mem_t[:, queries], rhs=k_t_plain[:, 0, keys], start=False, stop=True
+            )
+            nc.vector.tensor_reduce(
+                out=softmax_of[t]["row_max"][:, b : b + 1], in_=acc[:, :n], axis=AXIS.X, op=ALU.max
+            )
+            softmax_of[t]["banks"].append((acc, keys, n))
 
-            if n_banks == 2:
+        def exponentials(t):
+            sm = softmax_of[t]
+            if banks_of(t) == 2:
                 nc.vector.tensor_scalar(
-                    out=neg_max[:],
-                    in0=row_max[:, 0:1],
-                    scalar1=row_max[:, 1:2],
+                    out=sm["neg_max"][:],
+                    in0=sm["row_max"][:, 0:1],
+                    scalar1=sm["row_max"][:, 1:2],
                     scalar2=-SCALE,
                     op0=ALU.max,
                     op1=ALU.mult,
                 )
             else:
                 nc.vector.tensor_scalar(
-                    out=neg_max[:], in0=row_max[:, 0:1], scalar1=-SCALE, scalar2=None, op0=ALU.mult
+                    out=sm["neg_max"][:], in0=sm["row_max"][:, 0:1], scalar1=-SCALE, scalar2=None, op0=ALU.mult
                 )
-            for b, (acc, keys, n) in enumerate(banks):
+            for b, (acc, keys, n) in enumerate(sm["banks"]):
                 nc.scalar.activation(
-                    out=e_sb[:, keys],
+                    out=sm["e"][:, keys],
                     in_=acc[:, :n],
                     func=ACT.Exp,
-                    bias=neg_max[:, 0:1],
+                    bias=sm["neg_max"][:, 0:1],
                     scale=SCALE,
-                    accum_out=row_sum[:, b : b + 1],
+                    accum_out=sm["row_sum"][:, b : b + 1],
                 )
-            nc.vector.tensor_reduce(out=total[:], in_=row_sum[:, :n_banks], axis=AXIS.X, op=ALU.add)
-            nc.vector.reciprocal(out=rinv[:], in_=total[:])
-            e_of[t] = e_sb
-            rinv_of[t] = rinv
+
+            if banks_of(t) == 2:
+                nc.gpsimd.tensor_tensor(
+                    out=sm["total"][:], in0=sm["row_sum"][:, 0:1], in1=sm["row_sum"][:, 1:2], op=ALU.add
+                )
+                nc.gpsimd.tensor_tensor(out=sm["rinv"][:], in0=sm["total"][:], in1=minus_one[:], op=ALU.pow)
+            else:
+                nc.gpsimd.tensor_tensor(
+                    out=sm["rinv"][:], in0=sm["row_sum"][:, 0:1], in1=minus_one[:], op=ALU.pow
+                )
 
         rinv_rows_of = {}
 
         def transpose_e(t):
-            e_sb = e_of[t]
+            sm = softmax_of[t]
             bank = psum_transposes.tile([P, TILES, P], BF16, tag="transposes")
             for kt in range(t + 1):
-                nc.tensor.transpose(out=bank[:, kt, :], in_=e_sb[:, kt * P : (kt + 1) * P], identity=ident_bf16[:])
-            spread = psum_transposes.tile([P, P], F32, tag="transposes")
-            nc.tensor.transpose(out=spread[:], in_=rinv_of[t][:, 0:1].to_broadcast([P, P]), identity=ident_f32[:])
+                nc.tensor.transpose(
+                    out=bank[:, kt, :], in_=sm["e"][:, kt * P : (kt + 1) * P], identity=ident_bf16[:]
+                )
+            spread = psum_shared.tile([P, P], F32, tag="shared")
+            nc.tensor.transpose(out=spread[:], in_=sm["rinv"][:, 0:1].to_broadcast([P, P]), identity=ident_f32[:])
 
             first = first_slot(t)
             for g in range(passes_of(t)):
@@ -297,15 +343,12 @@ def tile_universalamrpalayer_pa_kernel(tc, q, k, v, mem, attention_mask, wo, bo,
 
         ctx_of = {}
 
-        def context(t):
-            rinv_rows = rinv_rows_of[t]
+        def context_products(t):
             ctx_grouped = per_tile.tile([P, E // K_PASS, P, PACK], BF16, align_bytes=64)
-            ctx_codes = per_tile.tile([P, E // K_PASS, P], U32, align_bytes=64)
-            ctx_scales = per_tile.tile([P, E // K_PASS, P], U8, align_bytes=64)
             first = first_slot(t)
             n_passes = passes_of(t)
             for g_out in range(E // K_PASS):
-                acc = psum_mx.tile([P, PACK, P], F32, tag="mx")
+                acc = psum_shared.tile([P, PACK, P], F32, tag="shared")
                 for j in range(PACK):
                     channels = slice((g_out * PACK + j) * P, (g_out * PACK + j + 1) * P)
                     for g in range(n_passes):
@@ -321,13 +364,18 @@ def tile_universalamrpalayer_pa_kernel(tc, q, k, v, mem, attention_mask, wo, bo,
                 nc.vector.tensor_tensor(
                     out=ctx_grouped[:, g_out, :, :],
                     in0=acc[:].rearrange("p j r -> p r j"),
-                    in1=rinv_rows[:].unsqueeze(2).to_broadcast([P, P, PACK]),
+                    in1=rinv_rows_of[t][:].unsqueeze(2).to_broadcast([P, P, PACK]),
                     op=ALU.mult,
                 )
+            ctx_of[t] = ctx_grouped
+
+        def quantise_context(t):
+            ctx_codes = per_tile.tile([P, E // K_PASS, P], U32, align_bytes=64)
+            ctx_scales = per_tile.tile([P, E // K_PASS, P], U8, align_bytes=64)
             nc.vector.quantize_mx(
                 out=ctx_codes[:].rearrange("p g r -> p (g r)").bitcast(FP8X4),
                 scales=ctx_scales[:].rearrange("p g r -> p (g r)"),
-                in_=ctx_grouped[:].rearrange("p g r j -> p (g r j)"),
+                in_=ctx_of[t][:].rearrange("p g r j -> p (g r j)"),
             )
             ctx_of[t] = (ctx_codes, ctx_scales)
 
@@ -336,7 +384,7 @@ def tile_universalamrpalayer_pa_kernel(tc, q, k, v, mem, attention_mask, wo, bo,
             out_sb = per_tile.tile([P, E], F32)
             for h in range(E // BANK):
                 cols = slice(h * BANK, (h + 1) * BANK)
-                acc = psum_mx.tile([P, BANK], F32, tag="mx")
+                acc = psum_shared.tile([P, BANK], F32, tag="shared")
                 for g in range(E // K_PASS):
                     nc.tensor.matmul_mx(
                         out=acc[:],
@@ -348,52 +396,41 @@ def tile_universalamrpalayer_pa_kernel(tc, q, k, v, mem, attention_mask, wo, bo,
                         stop=(g == E // K_PASS - 1),
                     )
                 nc.vector.tensor_tensor(out=out_sb[:, cols], in0=acc[:], in1=bias_rows[:, cols], op=ALU.add)
-            nc.sync.dma_start(out=out_rows[t], in_=out_sb[:])
+                nc.sync.dma_start(out=out_rows[t][:, cols], in_=out_sb[:, cols])
 
-        order = list(range(TILES - 1, -1, -1))
+        weight_passes = []
+        for g in range(S // K_PASS):
+            weight_passes.append((v_pieces[g], v_codes[:, g, :], v_scales[:, g, :]))
+        for g in range(E // K_PASS):
+            weight_passes.append((wo_pieces[g], wo_codes[:, g, :], wo_scales[:, g, :]))
+
+        spread_bias()
         transpose_queries(order[0])
-        for t in range(TILES):
-            transpose_keys(t)
+        for kt in range(BANK_TILES):
+            transpose_keys(kt)
         transpose_mem()
-        quantise_weight(v_pieces, v_codes, v_scales, nc.vector.tensor_copy)
-        for step in range(TILES + 2):
+        for step in range(TILES + PROJECT_LAG):
+            scoring = step < TILES
+            with_context = CONTEXT_LAG <= step < TILES + CONTEXT_LAG
+            if scoring:
+                start_softmax(order[step])
+                for b in range(banks_of(order[step]) - 1):
+                    score_bank(order[step], b)
             if step + 1 < TILES:
                 transpose_queries(order[step + 1])
-            if 1 <= step <= TILES:
-                transpose_e(order[step - 1])
-            if step < TILES:
-                scores_and_softmax(order[step])
-            if step == 1:
-                quantise_weight(wo_pieces, wo_codes, wo_scales, nc.scalar.copy)
-            if step >= 2:
-                project(order[step - 2])
-            if 1 <= step <= TILES:
-                context(order[step - 1])
-
-
-def passes_of(t):
-    return (t * P) // K_PASS + 1
-
-
-def first_slot(t):
-    return sum(passes_of(u) for u in range(t))
-
-
-def load_weight(nc, pool, passes):
-    pieces = []
-    for g in range(passes.shape[0]):
-        for h in range(passes.shape[3] // BANK):
-            cols = slice(h * BANK, (h + 1) * BANK)
-            raw = pool.tile([P, PACK, BANK], BF16, tag="weight_piece")
-            nc.sync.dma_start(out=raw[:], in_=passes[g][:, :, cols])
-            pieces.append((g, cols, raw))
-    return pieces
-
-
-def quantise_piece(nc, piece, codes, scales):
-    g, cols, grouped = piece
-    nc.vector.quantize_mx(
-        out=codes[:, g, cols].bitcast(FP8X4),
-        scales=scales[:, g, cols],
-        in_=grouped[:].rearrange("p c j -> p (c j)"),
-    )
+            if with_context:
+                transpose_e(order[step - CONTEXT_LAG])
+            if step == 0:
+                for kt in range(BANK_TILES, TILES):
+                    transpose_keys(kt)
+                quantise_weight(*weight_passes[0])
+            if scoring:
+                score_bank(order[step], banks_of(order[step]) - 1)
+                exponentials(order[step])
+            if step >= PROJECT_LAG:
+                project(order[step - PROJECT_LAG])
+            if with_context:
+                context_products(order[step - CONTEXT_LAG])
+                quantise_context(order[step - CONTEXT_LAG])
+            if step + 1 < len(weight_passes):
+                quantise_weight(*weight_passes[step + 1])

@@ -28,8 +28,10 @@ LAYER_DEPTH = 0.25
 MASKED = -1.0e30
 WORD_BLOCKS = 3
 PLAIN_BLOCKS = 2
-CONTEXT_LAG = 1
-PROJECT_LAG = 3
+E_LAG = 2
+CONTEXT_LAG = 3
+PROJECT_LAG = 6
+KEY_GROUP = 2
 
 QUERY_KEY_PAIRS = 512 * 512 + 512 * 1024
 FLOPS = 2 * QUERY_KEY_PAIRS * (E + DK + E) + 2 * S * E * E
@@ -61,7 +63,7 @@ def tile_universalamrpalayer_pa_kernel(tc, q, k, v, mem, attention_mask, wo, bo,
         keep = stack.enter_context(tc.tile_pool(name="keep", bufs=1))
         weights_in = stack.enter_context(tc.tile_pool(name="weights_in", bufs=8))
         weights_grouped = stack.enter_context(tc.tile_pool(name="weights_grouped", bufs=3))
-        per_tile = stack.enter_context(tc.tile_pool(name="per_tile", bufs=PROJECT_LAG + 1))
+        per_tile = stack.enter_context(tc.tile_pool(name="per_tile", bufs=3))
         psum_transposes = stack.enter_context(tc.psum_pool(name="psum_transposes", bufs=2))
         psum_scores = stack.enter_context(tc.psum_pool(name="psum_scores", bufs=3))
         psum_shared = stack.enter_context(tc.psum_pool(name="psum_shared", bufs=3))
@@ -104,10 +106,10 @@ def tile_universalamrpalayer_pa_kernel(tc, q, k, v, mem, attention_mask, wo, bo,
         nc.sync.dma_start(out=bias_row[0:1, :], in_=bo.unsqueeze(0))
         nc.sync.dma_start(out=q_raw[:, order[0], :], in_=q_rows[order[0]])
         nc.sync.dma_start(out=mask_row[0:1, :], in_=attention_mask)
-        for t in range(BANK_TILES):
+        for t in range(KEY_GROUP):
             nc.sync.dma_start(out=k_raw[:, t, :], in_=k_rows[t])
         nc.sync.dma_start(out=mem_raw[:], in_=mem_rows)
-        for t in range(BANK_TILES, TILES):
+        for t in range(KEY_GROUP, TILES):
             nc.sync.dma_start(out=k_raw[:, t, :], in_=k_rows[t])
         nc.sync.dma_start(out=q_raw[:, order[1], :], in_=q_rows[order[1]])
         v_pieces = load_weight(v_passes)
@@ -177,18 +179,14 @@ def tile_universalamrpalayer_pa_kernel(tc, q, k, v, mem, attention_mask, wo, bo,
             transpose_rows(k_raw[:, t, :], bank)
             keys = slice(t * P, (t + 1) * P)
             word_keys = slice(t * P // 2, (t + 1) * P // 2)
-            moves = (
-                (k_t_words[:, :, keys], bank[:, : WORD_BLOCKS * P].rearrange("p (w r) -> p w r", w=WORD_BLOCKS)),
-                (
-                    k_t_plain[:].bitcast(F32)[:, :, word_keys],
-                    bank[:, WORD_BLOCKS * P :].rearrange("p (h r) -> p h r", h=PLAIN_BLOCKS),
-                ),
+            nc.scalar.copy(
+                out=k_t_words[:, :, keys],
+                in_=bank[:, : WORD_BLOCKS * P].rearrange("p (w r) -> p w r", w=WORD_BLOCKS),
             )
-            for dst, src in moves:
-                if t % 2 == 0:
-                    nc.scalar.copy(out=dst, in_=src)
-                else:
-                    nc.vector.tensor_copy(out=dst, in_=src)
+            nc.scalar.copy(
+                out=k_t_plain[:].bitcast(F32)[:, :, word_keys],
+                in_=bank[:, WORD_BLOCKS * P :].rearrange("p (h r) -> p h r", h=PLAIN_BLOCKS),
+            )
 
         def transpose_mem():
             bank = psum_transposes.tile([P, TILES, P], BF16, tag="transposes")
@@ -237,21 +235,19 @@ def tile_universalamrpalayer_pa_kernel(tc, q, k, v, mem, attention_mask, wo, bo,
                 "banks": [],
             }
 
-        def score_bank(t, b):
-            lo = b * BANK
-            n = min(BANK, (t + 1) * P - lo)
+        def score_group(t, acc, lo, n):
             keys = slice(lo, lo + n)
+            end = lo % BANK + n
+            cols = slice(end - n, end)
             queries = slice(t * P, (t + 1) * P)
             q_words = q_t[:, t, : WORD_BLOCKS * P].bitcast(BF16).rearrange(
                 "p (w r e) -> p w r e", w=WORD_BLOCKS, e=2
             )
             q_plain = q_t[:, t, WORD_BLOCKS * P :].bitcast(BF16)
             k_words = k_t_words[:].bitcast(BF16).rearrange("p w (r e) -> p w r e", e=2)
-
-            acc = psum_scores.tile([P, BANK], F32, tag="scores")
             for h in range(PLAIN_BLOCKS):
                 nc.tensor.matmul(
-                    out=acc[:, :n],
+                    out=acc[:, cols],
                     lhsT=q_plain[:, h * P : (h + 1) * P],
                     rhs=k_t_plain[:, h, keys],
                     start=(h == 0),
@@ -260,22 +256,32 @@ def tile_universalamrpalayer_pa_kernel(tc, q, k, v, mem, attention_mask, wo, bo,
             for w in range(WORD_BLOCKS):
                 for half in range(2):
                     nc.tensor.matmul(
-                        out=acc[:, :n],
+                        out=acc[:, cols],
                         lhsT=q_words[:, w, :, half],
                         rhs=k_words[:, w, keys, half],
                         start=False,
                         stop=False,
                     )
-            nc.tensor.matmul(out=acc[:, :n], lhsT=unscale[:], rhs=mask_row[:, keys], start=False, stop=False)
-            if b == banks_of(t) - 1:
-                nc.tensor.matmul(out=acc[:, n - P : n], lhsT=ident_bf16[:], rhs=causal[:], start=False, stop=False)
+            nc.tensor.matmul(out=acc[:, cols], lhsT=unscale[:], rhs=mask_row[:, keys], start=False, stop=False)
+            if lo + n == (t + 1) * P:
+                nc.tensor.matmul(
+                    out=acc[:, end - P : end], lhsT=ident_bf16[:], rhs=causal[:], start=False, stop=False
+                )
             nc.tensor.matmul(
-                out=acc[:, :n], lhsT=mem_t[:, queries], rhs=k_t_plain[:, 0, keys], start=False, stop=True
+                out=acc[:, cols], lhsT=mem_t[:, queries], rhs=k_t_plain[:, 0, keys], start=False, stop=True
             )
+
+        def row_maximum(t, b, acc, n):
             nc.vector.tensor_reduce(
                 out=softmax_of[t]["row_max"][:, b : b + 1], in_=acc[:, :n], axis=AXIS.X, op=ALU.max
             )
-            softmax_of[t]["banks"].append((acc, keys, n))
+            softmax_of[t]["banks"].append((acc, slice(b * BANK, b * BANK + n), n))
+
+        def score_bank(t, b):
+            n = min(BANK, (t + 1) * P - b * BANK)
+            acc = psum_scores.tile([P, BANK], F32, tag="scores")
+            score_group(t, acc, b * BANK, n)
+            row_maximum(t, b, acc, n)
 
         def exponentials(t):
             sm = softmax_of[t]
@@ -370,8 +376,9 @@ def tile_universalamrpalayer_pa_kernel(tc, q, k, v, mem, attention_mask, wo, bo,
             ctx_of[t] = ctx_grouped
 
         def quantise_context(t):
-            ctx_codes = per_tile.tile([P, E // K_PASS, P], U32, align_bytes=64)
-            ctx_scales = per_tile.tile([P, E // K_PASS, P], U8, align_bytes=64)
+            waiting = PROJECT_LAG - CONTEXT_LAG + 1
+            ctx_codes = per_tile.tile([P, E // K_PASS, P], U32, align_bytes=64, bufs=waiting)
+            ctx_scales = per_tile.tile([P, E // K_PASS, P], U8, align_bytes=64, bufs=waiting)
             nc.vector.quantize_mx(
                 out=ctx_codes[:].rearrange("p g r -> p (g r)").bitcast(FP8X4),
                 scales=ctx_scales[:].rearrange("p g r -> p (g r)"),
@@ -384,7 +391,7 @@ def tile_universalamrpalayer_pa_kernel(tc, q, k, v, mem, attention_mask, wo, bo,
             out_sb = per_tile.tile([P, E], F32)
             for h in range(E // BANK):
                 cols = slice(h * BANK, (h + 1) * BANK)
-                acc = psum_shared.tile([P, BANK], F32, tag="shared")
+                acc = psum_scores.tile([P, BANK], F32, tag="scores")
                 for g in range(E // K_PASS):
                     nc.tensor.matmul_mx(
                         out=acc[:],
@@ -406,30 +413,42 @@ def tile_universalamrpalayer_pa_kernel(tc, q, k, v, mem, attention_mask, wo, bo,
 
         spread_bias()
         transpose_queries(order[0])
-        for kt in range(BANK_TILES):
+        for kt in range(KEY_GROUP):
             transpose_keys(kt)
         transpose_mem()
-        for step in range(TILES + PROJECT_LAG):
+        start_softmax(order[0])
+        groups_in_bank = BANK_TILES // KEY_GROUP
+        for b in range(banks_of(order[0])):
+            acc = psum_scores.tile([P, BANK], F32, tag="scores")
+            for g in range(b * groups_in_bank, (b + 1) * groups_in_bank):
+                if (g + 1) * KEY_GROUP < TILES:
+                    for kt in range((g + 1) * KEY_GROUP, (g + 2) * KEY_GROUP):
+                        transpose_keys(kt)
+                else:
+                    transpose_queries(order[1])
+                score_group(order[0], acc, g * KEY_GROUP * P, KEY_GROUP * P)
+            row_maximum(order[0], b, acc, BANK)
+            if b == 0:
+                quantise_weight(*weight_passes[0])
+        exponentials(order[0])
+        quantise_weight(*weight_passes[1])
+
+        for step in range(1, TILES + PROJECT_LAG):
             scoring = step < TILES
-            with_context = CONTEXT_LAG <= step < TILES + CONTEXT_LAG
             if scoring:
                 start_softmax(order[step])
                 for b in range(banks_of(order[step]) - 1):
                     score_bank(order[step], b)
             if step + 1 < TILES:
                 transpose_queries(order[step + 1])
-            if with_context:
-                transpose_e(order[step - CONTEXT_LAG])
-            if step == 0:
-                for kt in range(BANK_TILES, TILES):
-                    transpose_keys(kt)
-                quantise_weight(*weight_passes[0])
+            if E_LAG <= step < TILES + E_LAG:
+                transpose_e(order[step - E_LAG])
             if scoring:
                 score_bank(order[step], banks_of(order[step]) - 1)
                 exponentials(order[step])
             if step >= PROJECT_LAG:
                 project(order[step - PROJECT_LAG])
-            if with_context:
+            if CONTEXT_LAG <= step < TILES + CONTEXT_LAG:
                 context_products(order[step - CONTEXT_LAG])
                 quantise_context(order[step - CONTEXT_LAG])
             if step + 1 < len(weight_passes):

@@ -32,6 +32,7 @@ E_LAG = 2
 CONTEXT_LAG = 3
 PROJECT_LAG = 6
 KEY_GROUP = 2
+WARM_UP = 8
 
 QUERY_KEY_PAIRS = 512 * 512 + 512 * 1024
 FLOPS = 2 * QUERY_KEY_PAIRS * (E + DK + E) + 2 * S * E * E
@@ -103,11 +104,11 @@ def tile_universalamrpalayer_pa_kernel(tc, q, k, v, mem, attention_mask, wo, bo,
             return pieces
 
         order = list(range(TILES - 1, -1, -1))
-        nc.sync.dma_start(out=bias_row[0:1, :], in_=bo.unsqueeze(0))
         nc.sync.dma_start(out=q_raw[:, order[0], :], in_=q_rows[order[0]])
-        nc.sync.dma_start(out=mask_row[0:1, :], in_=attention_mask)
         for t in range(KEY_GROUP):
             nc.sync.dma_start(out=k_raw[:, t, :], in_=k_rows[t])
+        nc.sync.dma_start(out=mask_row[0:1, :], in_=attention_mask)
+        nc.sync.dma_start(out=bias_row[0:1, :], in_=bo.unsqueeze(0))
         nc.sync.dma_start(out=mem_raw[:], in_=mem_rows)
         for t in range(KEY_GROUP, TILES):
             nc.sync.dma_start(out=k_raw[:, t, :], in_=k_rows[t])
@@ -137,6 +138,8 @@ def tile_universalamrpalayer_pa_kernel(tc, q, k, v, mem, attention_mask, wo, bo,
         nc.gpsimd.tensor_copy(out=causal[:], in_=causal_f32[:])
         ones = keep.tile([P, P], BF16)
         nc.vector.memset(ones[:], 1.0)
+        warm_cols = keep.tile([P, BANK], BF16)
+        nc.vector.memset(warm_cols[:], 0.0)
         unscale = keep.tile([P, P], BF16)
         nc.vector.memset(unscale[:], 1.0 / SCALE)
         nc.vector.memset(e_grouped[:].bitcast(I32), 0)
@@ -145,6 +148,11 @@ def tile_universalamrpalayer_pa_kernel(tc, q, k, v, mem, attention_mask, wo, bo,
         warm = keep.tile([P, 1], F32)
         nc.vector.memset(warm[:], 0.0)
         nc.scalar.activation(out=warm[:], in_=warm[:], func=ACT.Exp)
+
+        def warm_up():
+            bank = psum_scores.tile([P, BANK], F32, tag="scores")
+            for i in range(WARM_UP):
+                nc.tensor.matmul(out=bank[:], lhsT=ones[:], rhs=warm_cols[:], start=True, stop=True)
 
         def spread_bias():
             for h in range(E // BANK):
@@ -411,11 +419,12 @@ def tile_universalamrpalayer_pa_kernel(tc, q, k, v, mem, attention_mask, wo, bo,
         for g in range(E // K_PASS):
             weight_passes.append((wo_pieces[g], wo_codes[:, g, :], wo_scales[:, g, :]))
 
-        spread_bias()
+        warm_up()
         transpose_queries(order[0])
         for kt in range(KEY_GROUP):
             transpose_keys(kt)
         transpose_mem()
+        spread_bias()
         start_softmax(order[0])
         groups_in_bank = BANK_TILES // KEY_GROUP
         for b in range(banks_of(order[0])):
@@ -446,10 +455,12 @@ def tile_universalamrpalayer_pa_kernel(tc, q, k, v, mem, attention_mask, wo, bo,
             if scoring:
                 score_bank(order[step], banks_of(order[step]) - 1)
                 exponentials(order[step])
+            with_context = CONTEXT_LAG <= step < TILES + CONTEXT_LAG
+            if with_context:
+                context_products(order[step - CONTEXT_LAG])
             if step >= PROJECT_LAG:
                 project(order[step - PROJECT_LAG])
-            if CONTEXT_LAG <= step < TILES + CONTEXT_LAG:
-                context_products(order[step - CONTEXT_LAG])
+            if with_context:
                 quantise_context(order[step - CONTEXT_LAG])
             if step + 1 < len(weight_passes):
                 quantise_weight(*weight_passes[step + 1])

@@ -46,6 +46,10 @@ def first_slot(t):
     return sum(passes_of(u) for u in range(t))
 
 
+def word_blocks_of(t):
+    return t // 2 + 1
+
+
 def banks_of(t):
     return t // BANK_TILES + 1
 
@@ -57,12 +61,12 @@ def tile_universalamrpalayer_pa_kernel(tc, q, k, v, mem, attention_mask, wo, bo,
     k_rows = k.flatten_outer_dims().rearrange("(t p) c -> t p c", p=P)
     mem_rows = mem.flatten_outer_dims().rearrange("(t p) c -> p t c", p=P)
     out_rows = out.flatten_outer_dims().rearrange("(t p) n -> t p n", p=P)
-    v_passes = v.flatten_outer_dims().rearrange("(g j p) c -> g p j c", j=PACK, p=P)
+    v_halves = v.flatten_outer_dims().rearrange("(g u p e) c -> g u p e c", u=2, p=P, e=2)
     wo_passes = wo.rearrange("(g j p) n -> g p j n", j=PACK, p=P)
 
     with ExitStack() as stack:
         keep = stack.enter_context(tc.tile_pool(name="keep", bufs=1))
-        weights_in = stack.enter_context(tc.tile_pool(name="weights_in", bufs=8))
+        weights_in = stack.enter_context(tc.tile_pool(name="weights_in", bufs=4))
         weights_grouped = stack.enter_context(tc.tile_pool(name="weights_grouped", bufs=3))
         per_tile = stack.enter_context(tc.tile_pool(name="per_tile", bufs=3))
         psum_transposes = stack.enter_context(tc.psum_pool(name="psum_transposes", bufs=2))
@@ -85,37 +89,44 @@ def tile_universalamrpalayer_pa_kernel(tc, q, k, v, mem, attention_mask, wo, bo,
         wo_codes = keep.tile([P, E // K_PASS, E], U32, align_bytes=64)
         wo_scales = keep.tile([P, E // K_PASS, E], U8, align_bytes=64)
         e_slots = first_slot(TILES)
-        e_grouped = keep.tile([P, e_slots, P, PACK], BF16, align_bytes=64)
+        e_grouped = keep.tile([P, e_slots, P, 2], F32, align_bytes=64)
         e_codes = keep.tile([P, e_slots, P], U32, align_bytes=64)
         e_scales = keep.tile([P, e_slots, P], U8, align_bytes=64)
 
         nc.gpsimd.memset(bias_row[:].bitcast(F32), 0.0)
         nc.vector.memset(mask_row[:].bitcast(I32), 0)
+        mask_diag = keep.tile([P, TILES, P], BF16)
+        nc.gpsimd.memset(mask_diag[:].bitcast(F32), 0.0)
 
-        def load_weight(passes):
-            pieces = []
-            for g in range(passes.shape[0]):
-                pieces.append([])
-                for h in range(passes.shape[3] // BANK):
-                    cols = slice(h * BANK, (h + 1) * BANK)
-                    raw = weights_in.tile([P, PACK, BANK], BF16, tag="weight_piece")
-                    nc.sync.dma_start(out=raw[:], in_=passes[g][:, :, cols])
-                    pieces[g].append((cols, raw))
-            return pieces
+        def load_v(g):
+            raw = weights_in.tile([P, PACK, E], BF16, tag="weight_pass")
+            for u in range(2):
+                nc.sync.dma_start(out=raw[:, 2 * u : 2 * u + 2, :], in_=v_halves[g][u])
+            return raw
+
+        def load_wo(g):
+            raw = weights_in.tile([P, PACK, E], BF16, tag="weight_pass")
+            for h in range(E // BANK):
+                cols = slice(h * BANK, (h + 1) * BANK)
+                nc.sync.dma_start(out=raw[:, :, cols], in_=wo_passes[g][:, :, cols])
+            return raw
 
         order = list(range(TILES - 1, -1, -1))
         nc.sync.dma_start(out=q_raw[:, order[0], :], in_=q_rows[order[0]])
         for t in range(KEY_GROUP):
             nc.sync.dma_start(out=k_raw[:, t, :], in_=k_rows[t])
-        nc.sync.dma_start(out=mask_row[0:1, :], in_=attention_mask)
+        nc.sync.dma_start(out=mask_row[P - 1 : P, :], in_=attention_mask)
         nc.sync.dma_start(out=bias_row[0:1, :], in_=bo.unsqueeze(0))
         nc.sync.dma_start(out=mem_raw[:], in_=mem_rows)
         for t in range(KEY_GROUP, TILES):
             nc.sync.dma_start(out=k_raw[:, t, :], in_=k_rows[t])
+        nc.sync.dma_start(
+            out=mask_diag[P - 1 : P, :, :], in_=attention_mask.rearrange("b (t r) -> b t r", r=P)
+        )
         nc.sync.dma_start(out=q_raw[:, order[1], :], in_=q_rows[order[1]])
-        v_pieces = load_weight(v_passes)
+        v_raw = [load_v(g) for g in range(S // K_PASS)]
         nc.sync.dma_start(out=q_raw[:, order[2], :], in_=q_rows[order[2]])
-        wo_pieces = load_weight(wo_passes)
+        wo_raw = [load_wo(g) for g in range(E // K_PASS)]
         for t in order[3:]:
             nc.sync.dma_start(out=q_raw[:, t, :], in_=q_rows[t])
 
@@ -123,28 +134,36 @@ def tile_universalamrpalayer_pa_kernel(tc, q, k, v, mem, attention_mask, wo, bo,
         make_identity(nc, ident_f32[:])
         ident_bf16 = keep.tile([P, P], BF16)
         make_identity(nc, ident_bf16[:])
-        causal_f32 = keep.tile([P, P], F32)
-        nc.gpsimd.memset(causal_f32[:], 0.0)
+        ident_mask = keep.tile([P, P], BF16)
+        make_identity(nc, ident_mask[:])
         nc.gpsimd.affine_select(
-            out=causal_f32[:],
-            in_=causal_f32[:],
+            out=ident_mask[:],
+            in_=ident_mask[:],
+            compare_op=ALU.is_ge,
+            fill=1.0 / SCALE,
+            base=P - 2,
+            pattern=[[0, P]],
+            channel_multiplier=-1,
+        )
+        nc.gpsimd.affine_select(
+            out=mask_diag[:],
+            in_=mask_diag[:],
             compare_op=ALU.is_ge,
             fill=MASKED,
             base=0,
-            pattern=[[-1, P]],
+            pattern=[[0, TILES], [-1, P]],
             channel_multiplier=1,
         )
-        causal = keep.tile([P, P], BF16)
-        nc.gpsimd.tensor_copy(out=causal[:], in_=causal_f32[:])
+        for t in range(TILES):
+            for g in range(passes_of(t)):
+                if word_blocks_of(t) - 2 * g < 2:
+                    nc.gpsimd.memset(e_grouped[:, first_slot(t) + g, :, :], 0.0)
         ones = keep.tile([P, P], BF16)
         nc.vector.memset(ones[:], 1.0)
         warm_cols = keep.tile([P, BANK], BF16)
         nc.vector.memset(warm_cols[:], 0.0)
-        unscale = keep.tile([P, P], BF16)
-        nc.vector.memset(unscale[:], 1.0 / SCALE)
-        nc.vector.memset(e_grouped[:].bitcast(I32), 0)
         minus_one = keep.tile([P, 1], F32)
-        nc.gpsimd.memset(minus_one[:], -1.0)
+        nc.vector.memset(minus_one[:], -1.0)
         warm = keep.tile([P, 1], F32)
         nc.vector.memset(warm[:], 0.0)
         nc.scalar.activation(out=warm[:], in_=warm[:], func=ACT.Exp)
@@ -208,13 +227,14 @@ def tile_universalamrpalayer_pa_kernel(tc, q, k, v, mem, attention_mask, wo, bo,
                 op0=ALU.mult,
             )
 
-        def quantise_weight(pieces, codes, scales):
+        def quantise_weight(raw, codes, scales):
             regrouped = []
-            for cols, raw in pieces:
+            for h in range(E // BANK):
+                cols = slice(h * BANK, (h + 1) * BANK)
                 grouped = weights_grouped.tile([P, BANK, PACK], BF16, align_bytes=64)
                 nc.vector.tensor_copy(
                     out=grouped[:].rearrange("p (c i) j -> p c j i", i=4),
-                    in_=raw[:].rearrange("p j (c i) -> p c j i", i=4),
+                    in_=raw[:, :, cols].rearrange("p j (c i) -> p c j i", i=4),
                 )
                 regrouped.append((cols, grouped))
             for cols, grouped in regrouped:
@@ -233,6 +253,8 @@ def tile_universalamrpalayer_pa_kernel(tc, q, k, v, mem, attention_mask, wo, bo,
             total = per_tile.tile([P, 1], F32)
             rinv = per_tile.tile([P, 1], F32)
             e_sb = per_tile.tile([P, S], BF16)
+            if t % 2 == 0:
+                nc.gpsimd.memset(e_sb[:, (t + 1) * P : (t + 2) * P].bitcast(F32), 0.0)
             softmax_of[t] = {
                 "row_max": row_max,
                 "neg_max": neg_max,
@@ -270,10 +292,19 @@ def tile_universalamrpalayer_pa_kernel(tc, q, k, v, mem, attention_mask, wo, bo,
                         start=False,
                         stop=False,
                     )
-            nc.tensor.matmul(out=acc[:, cols], lhsT=unscale[:], rhs=mask_row[:, keys], start=False, stop=False)
-            if lo + n == (t + 1) * P:
+            diagonal = lo + n == (t + 1) * P
+            before = n - P if diagonal else n
+            if before:
                 nc.tensor.matmul(
-                    out=acc[:, end - P : end], lhsT=ident_bf16[:], rhs=causal[:], start=False, stop=False
+                    out=acc[:, end - n : end - n + before],
+                    lhsT=ident_mask[:],
+                    rhs=mask_row[:, lo : lo + before],
+                    start=False,
+                    stop=False,
+                )
+            if diagonal:
+                nc.tensor.matmul(
+                    out=acc[:, end - P : end], lhsT=ident_mask[:], rhs=mask_diag[:, t, :], start=False, stop=False
                 )
             nc.tensor.matmul(
                 out=acc[:, cols], lhsT=mem_t[:, queries], rhs=k_t_plain[:, 0, keys], start=False, stop=True
@@ -330,20 +361,21 @@ def tile_universalamrpalayer_pa_kernel(tc, q, k, v, mem, attention_mask, wo, bo,
 
         def transpose_e(t):
             sm = softmax_of[t]
-            bank = psum_transposes.tile([P, TILES, P], BF16, tag="transposes")
-            for kt in range(t + 1):
+            bank = psum_transposes.tile([P, TILES // 2, P], F32, tag="transposes")
+            words = sm["e"][:].bitcast(F32)
+            for w in range(word_blocks_of(t)):
                 nc.tensor.transpose(
-                    out=bank[:, kt, :], in_=sm["e"][:, kt * P : (kt + 1) * P], identity=ident_bf16[:]
+                    out=bank[:, w, :], in_=words[:, w * P : (w + 1) * P], identity=ident_f32[:]
                 )
             spread = psum_shared.tile([P, P], F32, tag="shared")
             nc.tensor.transpose(out=spread[:], in_=sm["rinv"][:, 0:1].to_broadcast([P, P]), identity=ident_f32[:])
 
             first = first_slot(t)
             for g in range(passes_of(t)):
-                key_tiles = min(PACK, t + 1 - g * PACK)
+                blocks = min(2, word_blocks_of(t) - 2 * g)
                 nc.scalar.copy(
-                    out=e_grouped[:, first + g, :, :key_tiles],
-                    in_=bank[:, g * PACK : g * PACK + key_tiles, :].rearrange("p j r -> p r j"),
+                    out=e_grouped[:, first + g, :, :blocks],
+                    in_=bank[:, 2 * g : 2 * g + blocks, :].rearrange("p u r -> p r u"),
                 )
             rinv_rows = per_tile.tile([P, P], F32)
             nc.scalar.copy(out=rinv_rows[:], in_=spread[:])
@@ -352,7 +384,7 @@ def tile_universalamrpalayer_pa_kernel(tc, q, k, v, mem, attention_mask, wo, bo,
             nc.vector.quantize_mx(
                 out=e_codes[:, slots, :].rearrange("p s r -> p (s r)").bitcast(FP8X4),
                 scales=e_scales[:, slots, :].rearrange("p s r -> p (s r)"),
-                in_=e_grouped[:, slots, :, :].rearrange("p s r j -> p (s r j)"),
+                in_=e_grouped[:, slots, :, :].rearrange("p s r u -> p (s r u)").bitcast(BF16),
             )
 
         ctx_of = {}
@@ -415,9 +447,9 @@ def tile_universalamrpalayer_pa_kernel(tc, q, k, v, mem, attention_mask, wo, bo,
 
         weight_passes = []
         for g in range(S // K_PASS):
-            weight_passes.append((v_pieces[g], v_codes[:, g, :], v_scales[:, g, :]))
+            weight_passes.append((v_raw[g], v_codes[:, g, :], v_scales[:, g, :]))
         for g in range(E // K_PASS):
-            weight_passes.append((wo_pieces[g], wo_codes[:, g, :], wo_scales[:, g, :]))
+            weight_passes.append((wo_raw[g], wo_codes[:, g, :], wo_scales[:, g, :]))
 
         warm_up()
         transpose_queries(order[0])

@@ -162,8 +162,6 @@ def tile_universalamrpalayer_pa_kernel(tc, q, k, v, mem, attention_mask, wo, bo,
         nc.vector.memset(ones[:], 1.0)
         warm_cols = keep.tile([P, BANK], BF16)
         nc.vector.memset(warm_cols[:], 0.0)
-        minus_one = keep.tile([P, 1], F32)
-        nc.vector.memset(minus_one[:], -1.0)
         warm = keep.tile([P, 1], F32)
         nc.vector.memset(warm[:], 0.0)
         nc.scalar.activation(out=warm[:], in_=warm[:], func=ACT.Exp)
@@ -247,16 +245,14 @@ def tile_universalamrpalayer_pa_kernel(tc, q, k, v, mem, attention_mask, wo, bo,
         softmax_of = {}
 
         def start_softmax(t):
-            row_max = per_tile.tile([P, 2], F32)
-            neg_max = per_tile.tile([P, 1], F32)
+            neg_max = per_tile.tile([P, 2], F32)
             row_sum = per_tile.tile([P, 2], F32)
             total = per_tile.tile([P, 1], F32)
-            rinv = per_tile.tile([P, 1], F32)
+            rinv = per_tile.tile([P, 1], F32, bufs=CONTEXT_LAG + 1)
             e_sb = per_tile.tile([P, S], BF16)
             if t % 2 == 0:
                 nc.gpsimd.memset(e_sb[:, (t + 1) * P : (t + 2) * P].bitcast(F32), 0.0)
             softmax_of[t] = {
-                "row_max": row_max,
                 "neg_max": neg_max,
                 "row_sum": row_sum,
                 "total": total,
@@ -311,8 +307,16 @@ def tile_universalamrpalayer_pa_kernel(tc, q, k, v, mem, attention_mask, wo, bo,
             )
 
         def row_maximum(t, b, acc, n):
-            nc.vector.tensor_reduce(
-                out=softmax_of[t]["row_max"][:, b : b + 1], in_=acc[:, :n], axis=AXIS.X, op=ALU.max
+            neg_max = softmax_of[t]["neg_max"]
+            products = per_tile.tile([P, BANK], BF16)
+            nc.vector.tensor_scalar(
+                out=products[:, :n],
+                in0=acc[:, :n],
+                scalar1=-SCALE,
+                scalar2=None if b == 0 else neg_max[:, b - 1 : b],
+                op0=ALU.mult,
+                op1=ALU.min,
+                accum_out=neg_max[:, b : b + 1],
             )
             softmax_of[t]["banks"].append((acc, slice(b * BANK, b * BANK + n), n))
 
@@ -324,38 +328,26 @@ def tile_universalamrpalayer_pa_kernel(tc, q, k, v, mem, attention_mask, wo, bo,
 
         def exponentials(t):
             sm = softmax_of[t]
-            if banks_of(t) == 2:
-                nc.vector.tensor_scalar(
-                    out=sm["neg_max"][:],
-                    in0=sm["row_max"][:, 0:1],
-                    scalar1=sm["row_max"][:, 1:2],
-                    scalar2=-SCALE,
-                    op0=ALU.max,
-                    op1=ALU.mult,
-                )
-            else:
-                nc.vector.tensor_scalar(
-                    out=sm["neg_max"][:], in0=sm["row_max"][:, 0:1], scalar1=-SCALE, scalar2=None, op0=ALU.mult
-                )
             for b, (acc, keys, n) in enumerate(sm["banks"]):
                 nc.scalar.activation(
                     out=sm["e"][:, keys],
                     in_=acc[:, :n],
                     func=ACT.Exp,
-                    bias=sm["neg_max"][:, 0:1],
+                    bias=sm["neg_max"][:, banks_of(t) - 1 : banks_of(t)],
                     scale=SCALE,
                     accum_out=sm["row_sum"][:, b : b + 1],
                 )
 
             if banks_of(t) == 2:
-                nc.gpsimd.tensor_tensor(
-                    out=sm["total"][:], in0=sm["row_sum"][:, 0:1], in1=sm["row_sum"][:, 1:2], op=ALU.add
+                nc.scalar.activation(
+                    out=sm["total"][:], in_=sm["row_sum"][:, 0:1], func=ACT.Identity, bias=sm["row_sum"][:, 1:2]
                 )
-                nc.gpsimd.tensor_tensor(out=sm["rinv"][:], in0=sm["total"][:], in1=minus_one[:], op=ALU.pow)
-            else:
-                nc.gpsimd.tensor_tensor(
-                    out=sm["rinv"][:], in0=sm["row_sum"][:, 0:1], in1=minus_one[:], op=ALU.pow
-                )
+
+        def invert_sum(t):
+            sm = softmax_of[t]
+            nc.vector.reciprocal(
+                out=sm["rinv"][:], in_=sm["total"][:] if banks_of(t) == 2 else sm["row_sum"][:, 0:1]
+            )
 
         rinv_rows_of = {}
 
@@ -367,9 +359,6 @@ def tile_universalamrpalayer_pa_kernel(tc, q, k, v, mem, attention_mask, wo, bo,
                 nc.tensor.transpose(
                     out=bank[:, w, :], in_=words[:, w * P : (w + 1) * P], identity=ident_f32[:]
                 )
-            spread = psum_shared.tile([P, P], F32, tag="shared")
-            nc.tensor.transpose(out=spread[:], in_=sm["rinv"][:, 0:1].to_broadcast([P, P]), identity=ident_f32[:])
-
             first = first_slot(t)
             for g in range(passes_of(t)):
                 blocks = min(2, word_blocks_of(t) - 2 * g)
@@ -377,15 +366,21 @@ def tile_universalamrpalayer_pa_kernel(tc, q, k, v, mem, attention_mask, wo, bo,
                     out=e_grouped[:, first + g, :, :blocks],
                     in_=bank[:, 2 * g : 2 * g + blocks, :].rearrange("p u r -> p r u"),
                 )
-            rinv_rows = per_tile.tile([P, P], F32)
-            nc.scalar.copy(out=rinv_rows[:], in_=spread[:])
-            rinv_rows_of[t] = rinv_rows
             slots = slice(first, first + passes_of(t))
             nc.vector.quantize_mx(
                 out=e_codes[:, slots, :].rearrange("p s r -> p (s r)").bitcast(FP8X4),
                 scales=e_scales[:, slots, :].rearrange("p s r -> p (s r)"),
                 in_=e_grouped[:, slots, :, :].rearrange("p s r u -> p (s r u)").bitcast(BF16),
             )
+
+        def spread_inverse(t):
+            spread = psum_shared.tile([P, P], F32, tag="shared")
+            nc.tensor.transpose(
+                out=spread[:], in_=softmax_of[t]["rinv"][:, 0:1].to_broadcast([P, P]), identity=ident_f32[:]
+            )
+            rinv_rows = per_tile.tile([P, P], F32)
+            nc.scalar.copy(out=rinv_rows[:], in_=spread[:])
+            rinv_rows_of[t] = rinv_rows
 
         ctx_of = {}
 
@@ -482,8 +477,12 @@ def tile_universalamrpalayer_pa_kernel(tc, q, k, v, mem, attention_mask, wo, bo,
                     score_bank(order[step], b)
             if step + 1 < TILES:
                 transpose_queries(order[step + 1])
+            if step <= TILES:
+                invert_sum(order[step - 1])
             if E_LAG <= step < TILES + E_LAG:
                 transpose_e(order[step - E_LAG])
+            if CONTEXT_LAG <= step < TILES + CONTEXT_LAG:
+                spread_inverse(order[step - CONTEXT_LAG])
             if scoring:
                 score_bank(order[step], banks_of(order[step]) - 1)
                 exponentials(order[step])

@@ -2,7 +2,6 @@ import math
 from contextlib import ExitStack
 
 import concourse.mybir as mybir
-from concourse.masks import make_identity
 
 F32 = mybir.dt.float32
 BF16 = mybir.dt.bfloat16
@@ -93,10 +92,27 @@ def tile_universalamrpalayer_pa_kernel(tc, q, k, v, mem, attention_mask, wo, bo,
         e_codes = keep.tile([P, e_slots, P], U32, align_bytes=64)
         e_scales = keep.tile([P, e_slots, P], U8, align_bytes=64)
 
-        nc.gpsimd.memset(bias_row[:].bitcast(F32), 0.0)
+        ident_f32 = keep.tile([P, P], F32)
+        nc.vector.memset(ident_f32[:], 0.0)
+        nc.gpsimd.affine_select(
+            out=ident_f32[:],
+            in_=ident_f32[:],
+            compare_op=ALU.not_equal,
+            fill=1.0,
+            base=0,
+            pattern=[[-1, P]],
+            channel_multiplier=1,
+        )
+        ones = keep.tile([P, P], BF16)
+        nc.vector.memset(ones[:], 1.0)
+        warm_cols = keep.tile([P, BANK], BF16)
+        nc.vector.memset(warm_cols[:].bitcast(I32), 0)
         nc.vector.memset(mask_row[:].bitcast(I32), 0)
+        nc.vector.memset(bias_row[:].bitcast(I32), 0)
+        warm = keep.tile([P, 1], F32)
+        nc.vector.memset(warm[:], 0.0)
         mask_diag = keep.tile([P, TILES, P], BF16)
-        nc.gpsimd.memset(mask_diag[:].bitcast(F32), 0.0)
+        nc.vector.memset(mask_diag[:].bitcast(I32), 0)
 
         def load_v(g):
             raw = weights_in.tile([P, PACK, E], BF16, tag="weight_pass")
@@ -126,16 +142,14 @@ def tile_universalamrpalayer_pa_kernel(tc, q, k, v, mem, attention_mask, wo, bo,
         nc.sync.dma_start(out=q_raw[:, order[1], :], in_=q_rows[order[1]])
         v_raw = [load_v(g) for g in range(S // K_PASS)]
         nc.sync.dma_start(out=q_raw[:, order[2], :], in_=q_rows[order[2]])
-        wo_raw = [load_wo(g) for g in range(E // K_PASS)]
         for t in order[3:]:
             nc.sync.dma_start(out=q_raw[:, t, :], in_=q_rows[t])
+        wo_raw = [load_wo(g) for g in range(E // K_PASS)]
 
-        ident_f32 = keep.tile([P, P], F32)
-        make_identity(nc, ident_f32[:])
         ident_bf16 = keep.tile([P, P], BF16)
-        make_identity(nc, ident_bf16[:])
+        nc.vector.tensor_copy(out=ident_bf16[:], in_=ident_f32[:])
         ident_mask = keep.tile([P, P], BF16)
-        make_identity(nc, ident_mask[:])
+        nc.vector.tensor_copy(out=ident_mask[:], in_=ident_f32[:])
         nc.gpsimd.affine_select(
             out=ident_mask[:],
             in_=ident_mask[:],
@@ -158,12 +172,6 @@ def tile_universalamrpalayer_pa_kernel(tc, q, k, v, mem, attention_mask, wo, bo,
             for g in range(passes_of(t)):
                 if word_blocks_of(t) - 2 * g < 2:
                     nc.gpsimd.memset(e_grouped[:, first_slot(t) + g, :, :], 0.0)
-        ones = keep.tile([P, P], BF16)
-        nc.vector.memset(ones[:], 1.0)
-        warm_cols = keep.tile([P, BANK], BF16)
-        nc.vector.memset(warm_cols[:], 0.0)
-        warm = keep.tile([P, 1], F32)
-        nc.vector.memset(warm[:], 0.0)
         nc.scalar.activation(out=warm[:], in_=warm[:], func=ACT.Exp)
 
         def warm_up():

@@ -87,6 +87,7 @@ def tile_universalamrpalayer_pa_kernel(tc, q, k, v, mem, attention_mask, wo, bo,
         v_scales = keep.tile([P, S // K_PASS, E], U8, align_bytes=64)
         wo_codes = keep.tile([P, E // K_PASS, E], U32, align_bytes=64)
         wo_scales = keep.tile([P, E // K_PASS, E], U8, align_bytes=64)
+        e_all = keep.tile([P, TILES, S], BF16)
         e_slots = first_slot(TILES)
         e_grouped = keep.tile([P, e_slots, P, 2], F32, align_bytes=64)
         e_codes = keep.tile([P, e_slots, P], U32, align_bytes=64)
@@ -114,11 +115,8 @@ def tile_universalamrpalayer_pa_kernel(tc, q, k, v, mem, attention_mask, wo, bo,
         mask_diag = keep.tile([P, TILES, P], BF16)
         nc.vector.memset(mask_diag[:].bitcast(I32), 0)
 
-        def load_v(g):
-            raw = weights_in.tile([P, PACK, E], BF16, tag="weight_pass")
-            for u in range(2):
-                nc.sync.dma_start(out=raw[:, 2 * u : 2 * u + 2, :], in_=v_halves[g][u])
-            return raw
+        def load_v_half(g, u):
+            nc.sync.dma_start(out=v_raw[g][:, 2 * u : 2 * u + 2, :], in_=v_halves[g][u])
 
         def load_wo(g):
             raw = weights_in.tile([P, PACK, E], BF16, tag="weight_pass")
@@ -134,13 +132,20 @@ def tile_universalamrpalayer_pa_kernel(tc, q, k, v, mem, attention_mask, wo, bo,
         nc.sync.dma_start(out=mask_row[P - 1 : P, :], in_=attention_mask)
         nc.sync.dma_start(out=bias_row[0:1, :], in_=bo.unsqueeze(0))
         nc.sync.dma_start(out=mem_raw[:], in_=mem_rows)
+        v_raw = []
+        for g in range(S // K_PASS):
+            raw = weights_in.tile([P, PACK, E], BF16, tag="weight_pass")
+            v_raw.append(raw)
         for t in range(KEY_GROUP, TILES):
             nc.sync.dma_start(out=k_raw[:, t, :], in_=k_rows[t])
+            if t in (2, 4):
+                load_v_half(0, t // 2 - 1)
         nc.sync.dma_start(
             out=mask_diag[P - 1 : P, :, :], in_=attention_mask.rearrange("b (t r) -> b t r", r=P)
         )
         nc.sync.dma_start(out=q_raw[:, order[1], :], in_=q_rows[order[1]])
-        v_raw = [load_v(g) for g in range(S // K_PASS)]
+        for u in range(2):
+            load_v_half(1, u)
         nc.sync.dma_start(out=q_raw[:, order[2], :], in_=q_rows[order[2]])
         for t in order[3:]:
             nc.sync.dma_start(out=q_raw[:, t, :], in_=q_rows[t])
@@ -168,10 +173,12 @@ def tile_universalamrpalayer_pa_kernel(tc, q, k, v, mem, attention_mask, wo, bo,
             pattern=[[0, TILES], [-1, P]],
             channel_multiplier=1,
         )
+        for t in range(0, TILES, 2):
+            nc.vector.memset(e_all[:, t, (t + 1) * P : (t + 2) * P].bitcast(I32), 0)
         for t in range(TILES):
             for g in range(passes_of(t)):
                 if word_blocks_of(t) - 2 * g < 2:
-                    nc.gpsimd.memset(e_grouped[:, first_slot(t) + g, :, :], 0.0)
+                    nc.vector.memset(e_grouped[:, first_slot(t) + g, :, :], 0.0)
         nc.scalar.activation(out=warm[:], in_=warm[:], func=ACT.Exp)
 
         def warm_up():
@@ -233,7 +240,7 @@ def tile_universalamrpalayer_pa_kernel(tc, q, k, v, mem, attention_mask, wo, bo,
                 op0=ALU.mult,
             )
 
-        def quantise_weight(raw, codes, scales):
+        def regroup_weight(raw):
             regrouped = []
             for h in range(E // BANK):
                 cols = slice(h * BANK, (h + 1) * BANK)
@@ -243,12 +250,18 @@ def tile_universalamrpalayer_pa_kernel(tc, q, k, v, mem, attention_mask, wo, bo,
                     in_=raw[:, :, cols].rearrange("p j (c i) -> p c j i", i=4),
                 )
                 regrouped.append((cols, grouped))
+            return regrouped
+
+        def quantise_regrouped(regrouped, codes, scales):
             for cols, grouped in regrouped:
                 nc.vector.quantize_mx(
                     out=codes[:, cols].bitcast(FP8X4),
                     scales=scales[:, cols],
                     in_=grouped[:].rearrange("p c j -> p (c j)"),
                 )
+
+        def quantise_weight(raw, codes, scales):
+            quantise_regrouped(regroup_weight(raw), codes, scales)
 
         softmax_of = {}
 
@@ -257,15 +270,12 @@ def tile_universalamrpalayer_pa_kernel(tc, q, k, v, mem, attention_mask, wo, bo,
             row_sum = per_tile.tile([P, 2], F32)
             total = per_tile.tile([P, 1], F32)
             rinv = per_tile.tile([P, 1], F32, bufs=CONTEXT_LAG + 1)
-            e_sb = per_tile.tile([P, S], BF16)
-            if t % 2 == 0:
-                nc.gpsimd.memset(e_sb[:, (t + 1) * P : (t + 2) * P].bitcast(F32), 0.0)
             softmax_of[t] = {
                 "neg_max": neg_max,
                 "row_sum": row_sum,
                 "total": total,
                 "rinv": rinv,
-                "e": e_sb,
+                "e": e_all[:, t, :],
                 "banks": [],
             }
 
@@ -362,7 +372,7 @@ def tile_universalamrpalayer_pa_kernel(tc, q, k, v, mem, attention_mask, wo, bo,
         def transpose_e(t):
             sm = softmax_of[t]
             bank = psum_transposes.tile([P, TILES // 2, P], F32, tag="transposes")
-            words = sm["e"][:].bitcast(F32)
+            words = sm["e"].bitcast(F32)
             for w in range(word_blocks_of(t)):
                 nc.tensor.transpose(
                     out=bank[:, w, :], in_=words[:, w * P : (w + 1) * P], identity=ident_f32[:]
@@ -471,9 +481,11 @@ def tile_universalamrpalayer_pa_kernel(tc, q, k, v, mem, attention_mask, wo, bo,
                 else:
                     transpose_queries(order[1])
                 score_group(order[0], acc, g * KEY_GROUP * P, KEY_GROUP * P)
+            if b == 0:
+                first_pass = regroup_weight(v_raw[0])
             row_maximum(order[0], b, acc, BANK)
             if b == 0:
-                quantise_weight(*weight_passes[0])
+                quantise_regrouped(first_pass, *weight_passes[0][1:])
         exponentials(order[0])
         quantise_weight(*weight_passes[1])
 

@@ -31,7 +31,7 @@ E_LAG = 2
 CONTEXT_LAG = 3
 PROJECT_LAG = 6
 KEY_GROUP = 2
-WARM_UP = 8
+WARM_UP = 6
 
 QUERY_KEY_PAIRS = 512 * 512 + 512 * 1024
 FLOPS = 2 * QUERY_KEY_PAIRS * (E + DK + E) + 2 * S * E * E
@@ -77,12 +77,10 @@ def tile_universalamrpalayer_pa_kernel(tc, q, k, v, mem, attention_mask, wo, bo,
         k_raw = keep.tile([P, TILES, E], BF16)
         mem_raw = keep.tile([P, TILES, DK], BF16)
         q_t = keep.tile([P, TILES, BANK], F32)
-        k_t_words = keep.tile([P, WORD_BLOCKS, S], F32)
-        k_t_plain = keep.tile([P, PLAIN_BLOCKS, S], BF16)
+        k_t = keep.tile([P, TILES, BANK], F32)
         mem_t = keep.tile([P, S], BF16)
         mask_row = keep.tile([P, S], BF16)
-        bias_row = keep.tile([P, E], BF16)
-        bias_rows = keep.tile([P, E], F32)
+        bias_rows = keep.tile([P, E], BF16)
         v_codes = keep.tile([P, S // K_PASS, E], U32, align_bytes=64)
         v_scales = keep.tile([P, S // K_PASS, E], U8, align_bytes=64)
         wo_codes = keep.tile([P, E // K_PASS, E], U32, align_bytes=64)
@@ -109,7 +107,6 @@ def tile_universalamrpalayer_pa_kernel(tc, q, k, v, mem, attention_mask, wo, bo,
         warm_cols = keep.tile([P, BANK], BF16)
         nc.vector.memset(warm_cols[:].bitcast(I32), 0)
         nc.vector.memset(mask_row[:].bitcast(I32), 0)
-        nc.vector.memset(bias_row[:].bitcast(I32), 0)
         warm = keep.tile([P, 1], F32)
         nc.vector.memset(warm[:], 0.0)
         mask_diag = keep.tile([P, TILES, P], BF16)
@@ -130,7 +127,6 @@ def tile_universalamrpalayer_pa_kernel(tc, q, k, v, mem, attention_mask, wo, bo,
         for t in range(KEY_GROUP):
             nc.sync.dma_start(out=k_raw[:, t, :], in_=k_rows[t])
         nc.sync.dma_start(out=mask_row[P - 1 : P, :], in_=attention_mask)
-        nc.sync.dma_start(out=bias_row[0:1, :], in_=bo.unsqueeze(0))
         nc.sync.dma_start(out=mem_raw[:], in_=mem_rows)
         v_raw = []
         for g in range(S // K_PASS):
@@ -138,8 +134,8 @@ def tile_universalamrpalayer_pa_kernel(tc, q, k, v, mem, attention_mask, wo, bo,
             v_raw.append(raw)
         for t in range(KEY_GROUP, TILES):
             nc.sync.dma_start(out=k_raw[:, t, :], in_=k_rows[t])
-            if t in (2, 4):
-                load_v_half(0, t // 2 - 1)
+            if t in (5, 7):
+                load_v_half(0, (t - 5) // 2)
         nc.sync.dma_start(
             out=mask_diag[P - 1 : P, :, :], in_=attention_mask.rearrange("b (t r) -> b t r", r=P)
         )
@@ -150,6 +146,7 @@ def tile_universalamrpalayer_pa_kernel(tc, q, k, v, mem, attention_mask, wo, bo,
         for t in order[3:]:
             nc.sync.dma_start(out=q_raw[:, t, :], in_=q_rows[t])
         wo_raw = [load_wo(g) for g in range(E // K_PASS)]
+        nc.sync.dma_start(out=bias_rows[:], in_=bo.partition_broadcast(P))
 
         ident_bf16 = keep.tile([P, P], BF16)
         nc.vector.tensor_copy(out=ident_bf16[:], in_=ident_f32[:])
@@ -186,13 +183,6 @@ def tile_universalamrpalayer_pa_kernel(tc, q, k, v, mem, attention_mask, wo, bo,
             for i in range(WARM_UP):
                 nc.tensor.matmul(out=bank[:], lhsT=ones[:], rhs=warm_cols[:], start=True, stop=True)
 
-        def spread_bias():
-            for h in range(E // BANK):
-                cols = slice(h * BANK, (h + 1) * BANK)
-                bank = psum_shared.tile([P, BANK], F32, tag="shared")
-                nc.tensor.matmul(out=bank[:], lhsT=ones[:], rhs=bias_row[:, cols], start=True, stop=True)
-                nc.vector.tensor_copy(out=bias_rows[:, cols], in_=bank[:])
-
         def transpose_rows(rows, bank):
             words = rows.bitcast(F32)
             for w in range(WORD_BLOCKS):
@@ -217,16 +207,7 @@ def tile_universalamrpalayer_pa_kernel(tc, q, k, v, mem, attention_mask, wo, bo,
         def transpose_keys(t):
             bank = psum_shared.tile([P, BANK], F32, tag="shared")
             transpose_rows(k_raw[:, t, :], bank)
-            keys = slice(t * P, (t + 1) * P)
-            word_keys = slice(t * P // 2, (t + 1) * P // 2)
-            nc.scalar.copy(
-                out=k_t_words[:, :, keys],
-                in_=bank[:, : WORD_BLOCKS * P].rearrange("p (w r) -> p w r", w=WORD_BLOCKS),
-            )
-            nc.scalar.copy(
-                out=k_t_plain[:].bitcast(F32)[:, :, word_keys],
-                in_=bank[:, WORD_BLOCKS * P :].rearrange("p (h r) -> p h r", h=PLAIN_BLOCKS),
-            )
+            nc.scalar.copy(out=k_t[:, t, :], in_=bank[:])
 
         def transpose_mem():
             bank = psum_transposes.tile([P, TILES, P], BF16, tag="transposes")
@@ -280,7 +261,6 @@ def tile_universalamrpalayer_pa_kernel(tc, q, k, v, mem, attention_mask, wo, bo,
             }
 
         def score_group(t, acc, lo, n):
-            keys = slice(lo, lo + n)
             end = lo % BANK + n
             cols = slice(end - n, end)
             queries = slice(t * P, (t + 1) * P)
@@ -288,21 +268,26 @@ def tile_universalamrpalayer_pa_kernel(tc, q, k, v, mem, attention_mask, wo, bo,
                 "p (w r e) -> p w r e", w=WORD_BLOCKS, e=2
             )
             q_plain = q_t[:, t, WORD_BLOCKS * P :].bitcast(BF16)
-            k_words = k_t_words[:].bitcast(BF16).rearrange("p w (r e) -> p w r e", e=2)
+            key_tiles = slice(lo // P, (lo + n) // P)
+            k_words = k_t[:, key_tiles, : WORD_BLOCKS * P].bitcast(BF16).rearrange(
+                "p t (w r e) -> p t w r e", w=WORD_BLOCKS, e=2
+            )
+            k_plain = k_t[:, key_tiles, WORD_BLOCKS * P :].bitcast(BF16)
+            scores = acc[:, cols].rearrange("p (t r) -> p t r", r=P)
             for h in range(PLAIN_BLOCKS):
                 nc.tensor.matmul(
-                    out=acc[:, cols],
+                    out=scores,
                     lhsT=q_plain[:, h * P : (h + 1) * P],
-                    rhs=k_t_plain[:, h, keys],
+                    rhs=k_plain[:, :, h * P : (h + 1) * P],
                     start=(h == 0),
                     stop=False,
                 )
             for w in range(WORD_BLOCKS):
                 for half in range(2):
                     nc.tensor.matmul(
-                        out=acc[:, cols],
+                        out=scores,
                         lhsT=q_words[:, w, :, half],
-                        rhs=k_words[:, w, keys, half],
+                        rhs=k_words[:, :, w, :, half],
                         start=False,
                         stop=False,
                     )
@@ -320,9 +305,7 @@ def tile_universalamrpalayer_pa_kernel(tc, q, k, v, mem, attention_mask, wo, bo,
                 nc.tensor.matmul(
                     out=acc[:, end - P : end], lhsT=ident_mask[:], rhs=mask_diag[:, t, :], start=False, stop=False
                 )
-            nc.tensor.matmul(
-                out=acc[:, cols], lhsT=mem_t[:, queries], rhs=k_t_plain[:, 0, keys], start=False, stop=True
-            )
+            nc.tensor.matmul(out=scores, lhsT=mem_t[:, queries], rhs=k_plain[:, :, :P], start=False, stop=True)
 
         def row_maximum(t, b, acc, n):
             neg_max = softmax_of[t]["neg_max"]
@@ -469,7 +452,6 @@ def tile_universalamrpalayer_pa_kernel(tc, q, k, v, mem, attention_mask, wo, bo,
         for kt in range(KEY_GROUP):
             transpose_keys(kt)
         transpose_mem()
-        spread_bias()
         start_softmax(order[0])
         groups_in_bank = BANK_TILES // KEY_GROUP
         for b in range(banks_of(order[0])):

@@ -29,7 +29,8 @@ WORD_BLOCKS = 3
 PLAIN_BLOCKS = 2
 E_LAG = 2
 CONTEXT_LAG = 3
-PROJECT_LAG = 6
+PROJECT_LAG = 5
+FINAL_TILE = TILES // 2
 KEY_GROUP = 2
 WARM_UP = 6
 
@@ -117,12 +118,12 @@ def tile_universalamrpalayer_pa_kernel(tc, q, k, v, mem, attention_mask, wo, bo,
 
         def load_wo(g):
             raw = weights_in.tile([P, PACK, E], BF16, tag="weight_pass")
-            for h in range(E // BANK):
-                cols = slice(h * BANK, (h + 1) * BANK)
-                nc.sync.dma_start(out=raw[:, :, cols], in_=wo_passes[g][:, :, cols])
+            for half in range(2):
+                rows = slice(2 * half, 2 * half + 2)
+                nc.sync.dma_start(out=raw[:, rows, :], in_=wo_passes[g][:, rows, :])
             return raw
 
-        order = list(range(TILES - 1, -1, -1))
+        order = [t for t in range(TILES - 1, -1, -1) if t != FINAL_TILE] + [FINAL_TILE]
         nc.sync.dma_start(out=q_raw[:, order[0], :], in_=q_rows[order[0]])
         for t in range(KEY_GROUP):
             nc.sync.dma_start(out=k_raw[:, t, :], in_=k_rows[t])
@@ -143,9 +144,11 @@ def tile_universalamrpalayer_pa_kernel(tc, q, k, v, mem, attention_mask, wo, bo,
         for u in range(2):
             load_v_half(1, u)
         nc.sync.dma_start(out=q_raw[:, order[2], :], in_=q_rows[order[2]])
+        wo_raw = []
         for t in order[3:]:
             nc.sync.dma_start(out=q_raw[:, t, :], in_=q_rows[t])
-        wo_raw = [load_wo(g) for g in range(E // K_PASS)]
+            if t in (order[3], order[5]):
+                wo_raw.append(load_wo(len(wo_raw)))
         nc.sync.dma_start(out=bias_rows[:], in_=bo.partition_broadcast(P))
 
         ident_bf16 = keep.tile([P, P], BF16)

import math
from contextlib import ExitStack

import concourse.mybir as mybir

F32 = mybir.dt.float32
BF16 = mybir.dt.bfloat16
U32 = mybir.dt.uint32
U8 = mybir.dt.uint8
I32 = mybir.dt.int32
FP8X4 = mybir.dt.float8_e4m3fn_x4
ALU = mybir.AluOpType
ACT = mybir.ActivationFunctionType
AXIS = mybir.AxisListType

P = 128
S = 1024
E = 1024
DK = 128
TILES = S // P
PACK = 4
K_PASS = P * PACK
BANK = 512
BANK_TILES = BANK // P
SCALE = 1.0 / math.sqrt(64.0)
LAYER_DEPTH = 0.25
MASKED = -1.0e30
WORD_BLOCKS = 3
PLAIN_BLOCKS = 2
E_LAG = 2
CONTEXT_LAG = 3
PROJECT_LAG = 5
FINAL_TILE = TILES // 2
KEY_GROUP = 2
WARM_UP = 6

QUERY_KEY_PAIRS = 512 * 512 + 512 * 1024
FLOPS = 2 * QUERY_KEY_PAIRS * (E + DK + E) + 2 * S * E * E


def passes_of(t):
    return (t * P) // K_PASS + 1


def first_slot(t):
    return sum(passes_of(u) for u in range(t))


def word_blocks_of(t):
    return t // 2 + 1


def banks_of(t):
    return t // BANK_TILES + 1


def tile_universalamrpalayer_pa_kernel(tc, q, k, v, mem, attention_mask, wo, bo, out):
    nc = tc.nc

    q_rows = q.flatten_outer_dims().rearrange("(t p) c -> t p c", p=P)
    k_rows = k.flatten_outer_dims().rearrange("(t p) c -> t p c", p=P)
    mem_rows = mem.flatten_outer_dims().rearrange("(t p) c -> p t c", p=P)
    out_rows = out.flatten_outer_dims().rearrange("(t p) n -> t p n", p=P)
    v_halves = v.flatten_outer_dims().rearrange("(g u p e) c -> g u p e c", u=2, p=P, e=2)
    wo_passes = wo.rearrange("(g j p) n -> g p j n", j=PACK, p=P)

    with ExitStack() as stack:
        keep = stack.enter_context(tc.tile_pool(name="keep", bufs=1))
        weights_in = stack.enter_context(tc.tile_pool(name="weights_in", bufs=4))
        weights_grouped = stack.enter_context(tc.tile_pool(name="weights_grouped", bufs=3))
        per_tile = stack.enter_context(tc.tile_pool(name="per_tile", bufs=3))
        psum_transposes = stack.enter_context(tc.psum_pool(name="psum_transposes", bufs=2))
        psum_scores = stack.enter_context(tc.psum_pool(name="psum_scores", bufs=3))
        psum_shared = stack.enter_context(tc.psum_pool(name="psum_shared", bufs=3))
        stack.enter_context(tc.manual_schedule())

        q_raw = keep.tile([P, TILES, E], BF16)
        k_raw = keep.tile([P, TILES, E], BF16)
        mem_raw = keep.tile([P, TILES, DK], BF16)
        q_t = keep.tile([P, TILES, BANK], F32)
        k_t = keep.tile([P, TILES, BANK], F32)
        mem_t = keep.tile([P, S], BF16)
        mask_row = keep.tile([P, S], BF16)
        bias_rows = keep.tile([P, E], BF16)
        v_codes = keep.tile([P, S // K_PASS, E], U32, align_bytes=64)
        v_scales = keep.tile([P, S // K_PASS, E], U8, align_bytes=64)
        wo_codes = keep.tile([P, E // K_PASS, E], U32, align_bytes=64)
        wo_scales = keep.tile([P, E // K_PASS, E], U8, align_bytes=64)
        e_all = keep.tile([P, TILES, S], BF16)
        e_slots = first_slot(TILES)
        e_grouped = keep.tile([P, e_slots, P, 2], F32, align_bytes=64)
        e_codes = keep.tile([P, e_slots, P], U32, align_bytes=64)
        e_scales = keep.tile([P, e_slots, P], U8, align_bytes=64)

        ident_f32 = keep.tile([P, P], F32)
        nc.vector.memset(ident_f32[:], 0.0)
        nc.gpsimd.affine_select(
            out=ident_f32[:],
            in_=ident_f32[:],
            compare_op=ALU.not_equal,
            fill=1.0,
            base=0,
            pattern=[[-1, P]],
            channel_multiplier=1,
        )
        ones = keep.tile([P, P], BF16)
        nc.vector.memset(ones[:], 1.0)
        warm_cols = keep.tile([P, BANK], BF16)
        nc.vector.memset(warm_cols[:].bitcast(I32), 0)
        nc.vector.memset(mask_row[:].bitcast(I32), 0)
        warm = keep.tile([P, 1], F32)
        nc.vector.memset(warm[:], 0.0)
        mask_diag = keep.tile([P, TILES, P], BF16)
        nc.vector.memset(mask_diag[:].bitcast(I32), 0)

        def load_v_half(g, u):
            nc.sync.dma_start(out=v_raw[g][:, 2 * u : 2 * u + 2, :], in_=v_halves[g][u])

        def load_wo(g):
            raw = weights_in.tile([P, PACK, E], BF16, tag="weight_pass")
            for half in range(2):
                rows = slice(2 * half, 2 * half + 2)
                nc.sync.dma_start(out=raw[:, rows, :], in_=wo_passes[g][:, rows, :])
            return raw

        order = [t for t in range(TILES - 1, -1, -1) if t != FINAL_TILE] + [FINAL_TILE]
        nc.sync.dma_start(out=q_raw[:, order[0], :], in_=q_rows[order[0]])
        for t in range(KEY_GROUP):
            nc.sync.dma_start(out=k_raw[:, t, :], in_=k_rows[t])
        nc.sync.dma_start(out=mask_row[P - 1 : P, :], in_=attention_mask)
        nc.sync.dma_start(out=mem_raw[:], in_=mem_rows)
        v_raw = []
        for g in range(S // K_PASS):
            raw = weights_in.tile([P, PACK, E], BF16, tag="weight_pass")
            v_raw.append(raw)
        for t in range(KEY_GROUP, TILES):
            nc.sync.dma_start(out=k_raw[:, t, :], in_=k_rows[t])
            if t in (5, 7):
                load_v_half(0, (t - 5) // 2)
        nc.sync.dma_start(
            out=mask_diag[P - 1 : P, :, :], in_=attention_mask.rearrange("b (t r) -> b t r", r=P)
        )
        nc.sync.dma_start(out=q_raw[:, order[1], :], in_=q_rows[order[1]])
        for u in range(2):
            load_v_half(1, u)
        nc.sync.dma_start(out=q_raw[:, order[2], :], in_=q_rows[order[2]])
        wo_raw = []
        for t in order[3:]:
            nc.sync.dma_start(out=q_raw[:, t, :], in_=q_rows[t])
            if t in (order[3], order[5]):
                wo_raw.append(load_wo(len(wo_raw)))
        nc.sync.dma_start(out=bias_rows[:], in_=bo.partition_broadcast(P))

        ident_bf16 = keep.tile([P, P], BF16)
        nc.vector.tensor_copy(out=ident_bf16[:], in_=ident_f32[:])
        ident_mask = keep.tile([P, P], BF16)
        nc.vector.tensor_copy(out=ident_mask[:], in_=ident_f32[:])
        nc.gpsimd.affine_select(
            out=ident_mask[:],
            in_=ident_mask[:],
            compare_op=ALU.is_ge,
            fill=1.0 / SCALE,
            base=P - 2,
            pattern=[[0, P]],
            channel_multiplier=-1,
        )
        nc.gpsimd.affine_select(
            out=mask_diag[:],
            in_=mask_diag[:],
            compare_op=ALU.is_ge,
            fill=MASKED,
            base=0,
            pattern=[[0, TILES], [-1, P]],
            channel_multiplier=1,
        )
        for t in range(0, TILES, 2):
            nc.vector.memset(e_all[:, t, (t + 1) * P : (t + 2) * P].bitcast(I32), 0)
        for t in range(TILES):
            for g in range(passes_of(t)):
                if word_blocks_of(t) - 2 * g < 2:
                    nc.vector.memset(e_grouped[:, first_slot(t) + g, :, :], 0.0)
        nc.scalar.activation(out=warm[:], in_=warm[:], func=ACT.Exp)

        def warm_up():
            bank = psum_scores.tile([P, BANK], F32, tag="scores")
            for i in range(WARM_UP):
                nc.tensor.matmul(out=bank[:], lhsT=ones[:], rhs=warm_cols[:], start=True, stop=True)

        def transpose_rows(rows, bank):
            words = rows.bitcast(F32)
            for w in range(WORD_BLOCKS):
                nc.tensor.transpose(
                    out=bank[:, w * P : (w + 1) * P],
                    in_=words[:, (w + 1) * P : (w + 2) * P],
                    identity=ident_f32[:],
                )
            plain = bank[:, WORD_BLOCKS * P :].bitcast(BF16)
            for h in range(PLAIN_BLOCKS):
                nc.tensor.transpose(
                    out=plain[:, h * P : (h + 1) * P],
                    in_=rows[:, h * P : (h + 1) * P],
                    identity=ident_bf16[:],
                )

        def transpose_queries(t):
            bank = psum_transposes.tile([P, BANK], F32, tag="transposes")
            transpose_rows(q_raw[:, t, :], bank)
            nc.scalar.copy(out=q_t[:, t, :], in_=bank[:])

        def transpose_keys(t):
            bank = psum_shared.tile([P, BANK], F32, tag="shared")
            transpose_rows(k_raw[:, t, :], bank)
            nc.scalar.copy(out=k_t[:, t, :], in_=bank[:])

        def transpose_mem():
            bank = psum_transposes.tile([P, TILES, P], BF16, tag="transposes")
            for t in range(TILES):
                nc.tensor.transpose(out=bank[:, t, :], in_=mem_raw[:, t, :], identity=ident_bf16[:])
            nc.vector.tensor_scalar(
                out=mem_t[:],
                in0=bank[:].rearrange("p t r -> p (t r)"),
                scalar1=LAYER_DEPTH,
                scalar2=None,
                op0=ALU.mult,
            )

        def regroup_weight(raw):
            regrouped = []
            for h in range(E // BANK):
                cols = slice(h * BANK, (h + 1) * BANK)
                grouped = weights_grouped.tile([P, BANK, PACK], BF16, align_bytes=64)
                nc.vector.tensor_copy(
                    out=grouped[:].rearrange("p (c i) j -> p c j i", i=4),
                    in_=raw[:, :, cols].rearrange("p j (c i) -> p c j i", i=4),
                )
                regrouped.append((cols, grouped))
            return regrouped

        def quantise_regrouped(regrouped, codes, scales):
            for cols, grouped in regrouped:
                nc.vector.quantize_mx(
                    out=codes[:, cols].bitcast(FP8X4),
                    scales=scales[:, cols],
                    in_=grouped[:].rearrange("p c j -> p (c j)"),
                )

        def quantise_weight(raw, codes, scales):
            quantise_regrouped(regroup_weight(raw), codes, scales)

        softmax_of = {}

        def start_softmax(t):
            neg_max = per_tile.tile([P, 2], F32)
            row_sum = per_tile.tile([P, 2], F32)
            total = per_tile.tile([P, 1], F32)
            rinv = per_tile.tile([P, 1], F32, bufs=CONTEXT_LAG + 1)
            softmax_of[t] = {
                "neg_max": neg_max,
                "row_sum": row_sum,
                "total": total,
                "rinv": rinv,
                "e": e_all[:, t, :],
                "banks": [],
            }

        def score_group(t, acc, lo, n):
            end = lo % BANK + n
            cols = slice(end - n, end)
            queries = slice(t * P, (t + 1) * P)
            q_words = q_t[:, t, : WORD_BLOCKS * P].bitcast(BF16).rearrange(
                "p (w r e) -> p w r e", w=WORD_BLOCKS, e=2
            )
            q_plain = q_t[:, t, WORD_BLOCKS * P :].bitcast(BF16)
            key_tiles = slice(lo // P, (lo + n) // P)
            k_words = k_t[:, key_tiles, : WORD_BLOCKS * P].bitcast(BF16).rearrange(
                "p t (w r e) -> p t w r e", w=WORD_BLOCKS, e=2
            )
            k_plain = k_t[:, key_tiles, WORD_BLOCKS * P :].bitcast(BF16)
            scores = acc[:, cols].rearrange("p (t r) -> p t r", r=P)
            for h in range(PLAIN_BLOCKS):
                nc.tensor.matmul(
                    out=scores,
                    lhsT=q_plain[:, h * P : (h + 1) * P],
                    rhs=k_plain[:, :, h * P : (h + 1) * P],
                    start=(h == 0),
                    stop=False,
                )
            for w in range(WORD_BLOCKS):
                for half in range(2):
                    nc.tensor.matmul(
                        out=scores,
                        lhsT=q_words[:, w, :, half],
                        rhs=k_words[:, :, w, :, half],
                        start=False,
                        stop=False,
                    )
            diagonal = lo + n == (t + 1) * P
            before = n - P if diagonal else n
            if before:
                nc.tensor.matmul(
                    out=acc[:, end - n : end - n + before],
                    lhsT=ident_mask[:],
                    rhs=mask_row[:, lo : lo + before],
                    start=False,
                    stop=False,
                )
            if diagonal:
                nc.tensor.matmul(
                    out=acc[:, end - P : end], lhsT=ident_mask[:], rhs=mask_diag[:, t, :], start=False, stop=False
                )
            nc.tensor.matmul(out=scores, lhsT=mem_t[:, queries], rhs=k_plain[:, :, :P], start=False, stop=True)

        def row_maximum(t, b, acc, n):
            neg_max = softmax_of[t]["neg_max"]
            products = per_tile.tile([P, BANK], BF16)
            nc.vector.tensor_scalar(
                out=products[:, :n],
                in0=acc[:, :n],
                scalar1=-SCALE,
                scalar2=None if b == 0 else neg_max[:, b - 1 : b],
                op0=ALU.mult,
                op1=ALU.min,
                accum_out=neg_max[:, b : b + 1],
            )
            softmax_of[t]["banks"].append((acc, slice(b * BANK, b * BANK + n), n))

        def score_bank(t, b):
            n = min(BANK, (t + 1) * P - b * BANK)
            acc = psum_scores.tile([P, BANK], F32, tag="scores")
            score_group(t, acc, b * BANK, n)
            row_maximum(t, b, acc, n)

        def exponentials(t):
            sm = softmax_of[t]
            for b, (acc, keys, n) in enumerate(sm["banks"]):
                nc.scalar.activation(
                    out=sm["e"][:, keys],
                    in_=acc[:, :n],
                    func=ACT.Exp,
                    bias=sm["neg_max"][:, banks_of(t) - 1 : banks_of(t)],
                    scale=SCALE,
                    accum_out=sm["row_sum"][:, b : b + 1],
                )

            if banks_of(t) == 2:
                nc.scalar.activation(
                    out=sm["total"][:], in_=sm["row_sum"][:, 0:1], func=ACT.Identity, bias=sm["row_sum"][:, 1:2]
                )

        def invert_sum(t):
            sm = softmax_of[t]
            nc.vector.reciprocal(
                out=sm["rinv"][:], in_=sm["total"][:] if banks_of(t) == 2 else sm["row_sum"][:, 0:1]
            )

        rinv_rows_of = {}

        def transpose_e(t):
            sm = softmax_of[t]
            bank = psum_transposes.tile([P, TILES // 2, P], F32, tag="transposes")
            words = sm["e"].bitcast(F32)
            for w in range(word_blocks_of(t)):
                nc.tensor.transpose(
                    out=bank[:, w, :], in_=words[:, w * P : (w + 1) * P], identity=ident_f32[:]
                )
            first = first_slot(t)
            for g in range(passes_of(t)):
                blocks = min(2, word_blocks_of(t) - 2 * g)
                nc.scalar.copy(
                    out=e_grouped[:, first + g, :, :blocks],
                    in_=bank[:, 2 * g : 2 * g + blocks, :].rearrange("p u r -> p r u"),
                )
            slots = slice(first, first + passes_of(t))
            nc.vector.quantize_mx(
                out=e_codes[:, slots, :].rearrange("p s r -> p (s r)").bitcast(FP8X4),
                scales=e_scales[:, slots, :].rearrange("p s r -> p (s r)"),
                in_=e_grouped[:, slots, :, :].rearrange("p s r u -> p (s r u)").bitcast(BF16),
            )

        def spread_inverse(t):
            spread = psum_shared.tile([P, P], F32, tag="shared")
            nc.tensor.transpose(
                out=spread[:], in_=softmax_of[t]["rinv"][:, 0:1].to_broadcast([P, P]), identity=ident_f32[:]
            )
            rinv_rows = per_tile.tile([P, P], F32)
            nc.scalar.copy(out=rinv_rows[:], in_=spread[:])
            rinv_rows_of[t] = rinv_rows

        ctx_of = {}

        def context_products(t):
            ctx_grouped = per_tile.tile([P, E // K_PASS, P, PACK], BF16, align_bytes=64)
            first = first_slot(t)
            n_passes = passes_of(t)
            for g_out in range(E // K_PASS):
                acc = psum_shared.tile([P, PACK, P], F32, tag="shared")
                for j in range(PACK):
                    channels = slice((g_out * PACK + j) * P, (g_out * PACK + j + 1) * P)
                    for g in range(n_passes):
                        nc.tensor.matmul_mx(
                            out=acc[:, j, :],
                            lhsT=v_codes[:, g, channels].bitcast(FP8X4),
                            lhsT_scale=v_scales[:, g, channels],
                            rhs=e_codes[:, first + g, :].bitcast(FP8X4),
                            rhs_scale=e_scales[:, first + g, :],
                            start=(g == 0),
                            stop=(g == n_passes - 1),
                        )
                nc.vector.tensor_tensor(
                    out=ctx_grouped[:, g_out, :, :],
                    in0=acc[:].rearrange("p j r -> p r j"),
                    in1=rinv_rows_of[t][:].unsqueeze(2).to_broadcast([P, P, PACK]),
                    op=ALU.mult,
                )
            ctx_of[t] = ctx_grouped

        def quantise_context(t):
            waiting = PROJECT_LAG - CONTEXT_LAG + 1
            ctx_codes = per_tile.tile([P, E // K_PASS, P], U32, align_bytes=64, bufs=waiting)
            ctx_scales = per_tile.tile([P, E // K_PASS, P], U8, align_bytes=64, bufs=waiting)
            nc.vector.quantize_mx(
                out=ctx_codes[:].rearrange("p g r -> p (g r)").bitcast(FP8X4),
                scales=ctx_scales[:].rearrange("p g r -> p (g r)"),
                in_=ctx_of[t][:].rearrange("p g r j -> p (g r j)"),
            )
            ctx_of[t] = (ctx_codes, ctx_scales)

        def project(t):
            ctx_codes, ctx_scales = ctx_of[t]
            out_sb = per_tile.tile([P, E], F32)
            for h in range(E // BANK):
                cols = slice(h * BANK, (h + 1) * BANK)
                acc = psum_scores.tile([P, BANK], F32, tag="scores")
                for g in range(E // K_PASS):
                    nc.tensor.matmul_mx(
                        out=acc[:],
                        lhsT=ctx_codes[:, g, :].bitcast(FP8X4),
                        lhsT_scale=ctx_scales[:, g, :],
                        rhs=wo_codes[:, g, cols].bitcast(FP8X4),
                        rhs_scale=wo_scales[:, g, cols],
                        start=(g == 0),
                        stop=(g == E // K_PASS - 1),
                    )
                nc.vector.tensor_tensor(out=out_sb[:, cols], in0=acc[:], in1=bias_rows[:, cols], op=ALU.add)
                nc.sync.dma_start(out=out_rows[t][:, cols], in_=out_sb[:, cols])

        weight_passes = []
        for g in range(S // K_PASS):
            weight_passes.append((v_raw[g], v_codes[:, g, :], v_scales[:, g, :]))
        for g in range(E // K_PASS):
            weight_passes.append((wo_raw[g], wo_codes[:, g, :], wo_scales[:, g, :]))

        warm_up()
        transpose_queries(order[0])
        for kt in range(KEY_GROUP):
            transpose_keys(kt)
        transpose_mem()
        start_softmax(order[0])
        groups_in_bank = BANK_TILES // KEY_GROUP
        for b in range(banks_of(order[0])):
            acc = psum_scores.tile([P, BANK], F32, tag="scores")
            for g in range(b * groups_in_bank, (b + 1) * groups_in_bank):
                if (g + 1) * KEY_GROUP < TILES:
                    for kt in range((g + 1) * KEY_GROUP, (g + 2) * KEY_GROUP):
                        transpose_keys(kt)
                else:
                    transpose_queries(order[1])
                score_group(order[0], acc, g * KEY_GROUP * P, KEY_GROUP * P)
            if b == 0:
                first_pass = regroup_weight(v_raw[0])
            row_maximum(order[0], b, acc, BANK)
            if b == 0:
                quantise_regrouped(first_pass, *weight_passes[0][1:])
        exponentials(order[0])
        quantise_weight(*weight_passes[1])

        for step in range(1, TILES + PROJECT_LAG):
            scoring = step < TILES
            if scoring:
                start_softmax(order[step])
                for b in range(banks_of(order[step]) - 1):
                    score_bank(order[step], b)
            if step + 1 < TILES:
                transpose_queries(order[step + 1])
            if step <= TILES:
                invert_sum(order[step - 1])
            if E_LAG <= step < TILES + E_LAG:
                transpose_e(order[step - E_LAG])
            if CONTEXT_LAG <= step < TILES + CONTEXT_LAG:
                spread_inverse(order[step - CONTEXT_LAG])
            if scoring:
                score_bank(order[step], banks_of(order[step]) - 1)
                exponentials(order[step])
            with_context = CONTEXT_LAG <= step < TILES + CONTEXT_LAG
            if with_context:
                context_products(order[step - CONTEXT_LAG])
            if step >= PROJECT_LAG:
                project(order[step - PROJECT_LAG])
            if with_context:
                quantise_context(order[step - CONTEXT_LAG])
            if step + 1 < len(weight_passes):
                quantise_weight(*weight_passes[step + 1])
